import numpy as np
import ml_dtypes


def mxq(x, axis, fmt="e4m3"):
    dtype, down = {"e4m3": (ml_dtypes.float8_e4m3fn, 7), "e5m2": (ml_dtypes.float8_e5m2, 14)}[fmt]
    v = np.moveaxis(np.asarray(x, np.float32).astype(ml_dtypes.bfloat16).astype(np.float64), axis, -1)
    blocks = v.reshape(v.shape[:-1] + (-1, 32))
    amax = np.abs(blocks).max(-1, keepdims=True)
    byte = np.maximum(np.where(amax > 0, np.frexp(amax)[1] - 1 + 127, 0) - down, 1)
    scale = np.exp2(byte - 127.0)
    codes = (blocks / scale).astype(np.float32).astype(dtype).astype(np.float64)
    return np.moveaxis((codes * scale).reshape(v.shape), -1, axis)


WIDE = False


def mx_kscale(k):
    if not WIDE:
        return np.ones(k)
    levels = np.array([10, -10, 5, -5, 0])
    a = np.random.permutation(np.resize(levels, k // 512 * 4)).reshape(k // 512, 4)
    idx = np.arange(k)
    return np.exp2(a[idx // 512, idx % 128 // 32])


BF16 = ml_dtypes.bfloat16


def bf(x):
    return np.asarray(x, np.float32).astype(BF16)


def f64(x):
    return np.asarray(x).astype(np.float64)


B, C, HID, HS = 4, 512, 1024, 32
HH = HID // 2
CIN2 = HID + HH
P = HS * HS


def setup_inputs():
    s, t = mx_kscale(C), mx_kscale(HID)
    u = np.concatenate([t, t[HH:]])
    return {"x": bf(np.random.standard_normal((B, C, HS, HS)) * s[None, :, None, None]),
            "w1": bf(np.random.standard_normal((C, HID)) / np.sqrt(C) / s[:, None] * t),
            "b1": bf(np.random.standard_normal(HID) * 0.2 * t),
            "w2": bf(np.random.standard_normal((CIN2, C)) / np.sqrt(CIN2) / u[:, None]),
            "b2": bf(np.random.standard_normal(C) * 0.2)}


def reference(x, w1, b1, w2, b2):
    xq = mxq(f64(x).reshape(B, C, P), 1, "e4m3")
    y = (mxq(f64(w1), 0, "e4m3").T @ xq) + f64(b1)[None, :, None]
    a, fmap = np.split(y, 2, axis=1)
    z = np.concatenate([a, fmap, np.maximum(fmap, 0.0)], axis=1)
    o = (mxq(f64(w2), 0, "e4m3").T @ mxq(z, 1, "e4m3")) + f64(b2)[None, :, None]
    return o.reshape(B, C, HS, HS)

@@ -1,0 +1,190 @@
+from contextlib import ExitStack
+
+import concourse.mybir as mybir
+
+BF16 = mybir.dt.bfloat16
+F32 = mybir.dt.float32
+U32 = mybir.dt.uint32
+U8 = mybir.dt.uint8
+FP8X4 = mybir.dt.float8_e4m3fn_x4
+ADD = mybir.AluOpType.add
+IDENTITY = mybir.ActivationFunctionType.Identity
+
+P = 128
+PACK = 4
+K_PASS = P * PACK
+
+IMAGES = 4
+C_IN = 512
+HIDDEN = 1024
+PIXELS = 1024
+C_OUT = 512
+Y_GROUPS = HIDDEN // K_PASS
+Z_GROUPS = Y_GROUPS + 1
+BLOCK = 512
+QUAD = BLOCK // PACK
+BLOCKS_PER_IMAGE = PIXELS // BLOCK
+
+FLOPS = 2 * IMAGES * PIXELS * (C_IN * HIDDEN + Z_GROUPS * K_PASS * C_OUT)
+
+
+def regroup_pixels(copy, grouped, rows):
+    copy(
+        out=grouped.rearrange("p (c i) t -> p c t i", i=PACK),
+        in_=rows.rearrange("p t (c i) -> p c t i", i=PACK),
+    )
+
+
+def regroup_weight(copy, grouped, rows):
+    copy(
+        out=grouped.rearrange("p a q t -> p q t a"),
+        in_=rows.rearrange("p t (q a) -> p q t a", a=PACK),
+    )
+
+
+def tile_offm_pa_t_kernel(tc, x, w1, b1, w2, b2, out):
+    nc = tc.nc
+    with ExitStack() as ctx:
+        keep = ctx.enter_context(tc.tile_pool(name="keep", bufs=1))
+        wstage = ctx.enter_context(tc.tile_pool(name="wstage", bufs=2))
+        xstage = ctx.enter_context(tc.tile_pool(name="xstage", bufs=2))
+        zstage = ctx.enter_context(tc.tile_pool(name="zstage", bufs=2))
+        ostage = ctx.enter_context(tc.tile_pool(name="ostage", bufs=3))
+        y_psum = ctx.enter_context(tc.psum_pool(name="y_psum", bufs=4))
+        o_psum = ctx.enter_context(tc.psum_pool(name="o_psum", bufs=1))
+
+        x_rows = x.rearrange("b (p t) h w -> b p t (h w)", t=PACK)
+        w1_rows = w1.rearrange("(p t) d -> p t d", t=PACK)
+        w2_rows = w2.rearrange("(g p t) e -> g p t e", g=Z_GROUPS, t=PACK)
+        out_rows = out.rearrange("b (p m) h w -> b p m (h w)", m=PACK)
+
+        b1_bf = keep.tile([P, Y_GROUPS, PACK], BF16)
+        nc.scalar.dma_start(out=b1_bf[:], in_=b1.rearrange("(g p a) -> p g a", g=Y_GROUPS, a=PACK))
+        b2_bf = keep.tile([P, PACK], BF16)
+        nc.scalar.dma_start(out=b2_bf[:], in_=b2.rearrange("(p m) -> p m", m=PACK))
+
+        w1_raw = keep.tile([P, PACK, HIDDEN], BF16)
+        w2_raw = keep.tile([P, Z_GROUPS, PACK, C_OUT], BF16)
+        x_raw = [keep.tile([P, PACK, PIXELS], BF16, name="x_raw%d" % b) for b in range(IMAGES)]
+
+        nc.sync.dma_start(out=x_raw[0][:, :, 0:BLOCK], in_=x_rows[0][:, :, 0:BLOCK])
+        nc.sync.dma_start(out=w1_raw[:, :, 0:K_PASS], in_=w1_rows[:, :, 0:K_PASS])
+        nc.sync.dma_start(out=w1_raw[:, :, K_PASS:HIDDEN], in_=w1_rows[:, :, K_PASS:HIDDEN])
+        nc.sync.dma_start(out=x_raw[0][:, :, BLOCK:PIXELS], in_=x_rows[0][:, :, BLOCK:PIXELS])
+        for g in range(Z_GROUPS):
+            nc.sync.dma_start(out=w2_raw[:, g], in_=w2_rows[g])
+        for b in range(1, IMAGES):
+            nc.sync.dma_start(out=x_raw[b][:], in_=x_rows[b])
+
+        b1_f = keep.tile([P, Y_GROUPS, PACK], F32)
+        nc.vector.tensor_copy(out=b1_f[:], in_=b1_bf[:])
+        b2_f = keep.tile([P, PACK], F32)
+        nc.vector.tensor_copy(out=b2_f[:], in_=b2_bf[:])
+
+        w1_codes = keep.tile([P, Y_GROUPS, K_PASS], U32, align_bytes=64)
+        w1_scales = keep.tile([P, Y_GROUPS, K_PASS], U8, align_bytes=64)
+        w2_codes = keep.tile([P, Z_GROUPS, C_OUT], U32, align_bytes=64)
+        w2_scales = keep.tile([P, Z_GROUPS, C_OUT], U8, align_bytes=64)
+
+        def quantise_x(block):
+            b, half = divmod(block, BLOCKS_PER_IMAGE)
+            cols = slice(half * BLOCK, (half + 1) * BLOCK)
+            x_grouped = xstage.tile([P, BLOCK, PACK], BF16, align_bytes=64)
+            regroup_pixels(nc.scalar.copy, x_grouped[:], x_raw[b][:, :, cols])
+            x_codes = xstage.tile([P, BLOCK], U32, align_bytes=64)
+            x_scales = xstage.tile([P, BLOCK], U8, align_bytes=64)
+            nc.vector.quantize_mx(
+                out=x_codes[:].bitcast(FP8X4),
+                scales=x_scales[:],
+                in_=x_grouped[:].rearrange("p n t -> p (n t)"),
+            )
+            return x_codes, x_scales
+
+        def quantise_weight(copy, rows, codes, scales):
+            w_grouped = wstage.tile([P, PACK, P, PACK], BF16, align_bytes=64)
+            regroup_weight(copy, w_grouped[:], rows)
+            nc.vector.quantize_mx(
+                out=codes.bitcast(FP8X4),
+                scales=scales,
+                in_=w_grouped[:].rearrange("p a q t -> p (a q t)"),
+            )
+
+        next_x = quantise_x(0)
+        for g in range(Y_GROUPS):
+            quantise_weight(
+                nc.vector.tensor_copy,
+                w1_raw[:, :, g * K_PASS : (g + 1) * K_PASS],
+                w1_codes[:, g, :],
+                w1_scales[:, g, :],
+            )
+
+        for block in range(IMAGES * BLOCKS_PER_IMAGE):
+            b, half = divmod(block, BLOCKS_PER_IMAGE)
+            x_codes, x_scales = next_x
+            if block + 1 < IMAGES * BLOCKS_PER_IMAGE:
+                next_x = quantise_x(block + 1)
+            if block == 0:
+                for g in range(Z_GROUPS):
+                    quantise_weight(nc.scalar.copy, w2_raw[:, g], w2_codes[:, g, :], w2_scales[:, g, :])
+
+            z = zstage.tile([P, Z_GROUPS, BLOCK, PACK], BF16, align_bytes=64)
+            z_codes = zstage.tile([P, Z_GROUPS, BLOCK], U32, align_bytes=64)
+            z_scales = zstage.tile([P, Z_GROUPS, BLOCK], U8, align_bytes=64)
+
+            def quantise_z(g):
+                nc.vector.quantize_mx(
+                    out=z_codes[:, g, :].bitcast(FP8X4),
+                    scales=z_scales[:, g, :],
+                    in_=z[:, g].rearrange("p n t -> p (n t)"),
+                )
+
+            for g in range(Y_GROUPS):
+                for quad in range(PACK):
+                    cols = slice(quad * QUAD, (quad + 1) * QUAD)
+                    y = y_psum.tile([P, PACK, QUAD], F32)
+                    for a in range(PACK):
+                        w_cols = slice(a * P, (a + 1) * P)
+                        nc.tensor.matmul_mx(
+                            out=y[:, a, :],
+                            lhsT=w1_codes[:, g, w_cols].bitcast(FP8X4),
+                            lhsT_scale=w1_scales[:, g, w_cols],
+                            rhs=x_codes[:, cols].bitcast(FP8X4),
+                            rhs_scale=x_scales[:, cols],
+                            start=True,
+                            stop=True,
+                        )
+                    nc.vector.tensor_tensor(
+                        out=z[:, g, cols, :],
+                        in0=y[:].rearrange("p a n -> p n a"),
+                        in1=b1_f[:, g, :].unsqueeze(1).to_broadcast([P, QUAD, PACK]),
+                        op=ADD,
+                    )
+                quantise_z(g)
+            nc.vector.tensor_scalar_max(
+                out=z[:, 2].rearrange("p n t -> p (n t)"),
+                in0=z[:, 1].rearrange("p n t -> p (n t)"),
+                scalar1=0.0,
+            )
+            quantise_z(2)
+
+            acc = [o_psum.tile([P, BLOCK], F32, name="acc%d" % m) for m in range(PACK)]
+            for g in range(Z_GROUPS):
+                for m in range(PACK):
+                    w_cols = slice(m * P, (m + 1) * P)
+                    nc.tensor.matmul_mx(
+                        out=acc[m][:],
+                        lhsT=w2_codes[:, g, w_cols].bitcast(FP8X4),
+                        lhsT_scale=w2_scales[:, g, w_cols],
+                        rhs=z_codes[:, g, :].bitcast(FP8X4),
+                        rhs_scale=z_scales[:, g, :],
+                        start=(g == 0),
+                        stop=(g == Z_GROUPS - 1),
+                    )
+            result = ostage.tile([P, PACK, BLOCK], F32)
+            for m in range(PACK):
+                nc.scalar.activation(
+                    out=result[:, m, :], in_=acc[m][:], func=IDENTITY, bias=b2_f[:, m : m + 1], scale=1.0
+                )
+            nc.sync.dma_start(
+                out=out_rows[b][:, :, half * BLOCK : (half + 1) * BLOCK], in_=result[:]
+            )

@@ -21,9 +21,12 @@ PIXELS = 1024
 C_OUT = 512
 Y_GROUPS = HIDDEN // K_PASS
 Z_GROUPS = Y_GROUPS + 1
+A, FMAP, RELU = 0, 1, 2
 BLOCK = 512
 QUAD = BLOCK // PACK
+HALF = BLOCK // 2
 BLOCKS_PER_IMAGE = PIXELS // BLOCK
+N_BLOCKS = IMAGES * BLOCKS_PER_IMAGE
 
 FLOPS = 2 * IMAGES * PIXELS * (C_IN * HIDDEN + Z_GROUPS * K_PASS * C_OUT)
 
@@ -46,12 +49,12 @@ def tile_offm_pa_t_kernel(tc, x, w1, b1, w2, b2, out):
     nc = tc.nc
     with ExitStack() as ctx:
         keep = ctx.enter_context(tc.tile_pool(name="keep", bufs=1))
-        wstage = ctx.enter_context(tc.tile_pool(name="wstage", bufs=2))
         xstage = ctx.enter_context(tc.tile_pool(name="xstage", bufs=2))
         zstage = ctx.enter_context(tc.tile_pool(name="zstage", bufs=2))
-        ostage = ctx.enter_context(tc.tile_pool(name="ostage", bufs=3))
+        ostage = ctx.enter_context(tc.tile_pool(name="ostage", bufs=8))
         y_psum = ctx.enter_context(tc.psum_pool(name="y_psum", bufs=4))
         o_psum = ctx.enter_context(tc.psum_pool(name="o_psum", bufs=1))
+        ctx.enter_context(tc.manual_schedule())
 
         x_rows = x.rearrange("b (p t) h w -> b p t (h w)", t=PACK)
         w1_rows = w1.rearrange("(p t) d -> p t d", t=PACK)
@@ -59,132 +62,236 @@ def tile_offm_pa_t_kernel(tc, x, w1, b1, w2, b2, out):
         out_rows = out.rearrange("b (p m) h w -> b p m (h w)", m=PACK)
 
         b1_bf = keep.tile([P, Y_GROUPS, PACK], BF16)
-        nc.scalar.dma_start(out=b1_bf[:], in_=b1.rearrange("(g p a) -> p g a", g=Y_GROUPS, a=PACK))
         b2_bf = keep.tile([P, PACK], BF16)
-        nc.scalar.dma_start(out=b2_bf[:], in_=b2.rearrange("(p m) -> p m", m=PACK))
-
-        w1_raw = keep.tile([P, PACK, HIDDEN], BF16)
-        w2_raw = keep.tile([P, Z_GROUPS, PACK, C_OUT], BF16)
-        x_raw = [keep.tile([P, PACK, PIXELS], BF16, name="x_raw%d" % b) for b in range(IMAGES)]
-
-        nc.sync.dma_start(out=x_raw[0][:, :, 0:BLOCK], in_=x_rows[0][:, :, 0:BLOCK])
-        nc.sync.dma_start(out=w1_raw[:, :, 0:K_PASS], in_=w1_rows[:, :, 0:K_PASS])
-        nc.sync.dma_start(out=w1_raw[:, :, K_PASS:HIDDEN], in_=w1_rows[:, :, K_PASS:HIDDEN])
-        nc.sync.dma_start(out=x_raw[0][:, :, BLOCK:PIXELS], in_=x_rows[0][:, :, BLOCK:PIXELS])
-        for g in range(Z_GROUPS):
-            nc.sync.dma_start(out=w2_raw[:, g], in_=w2_rows[g])
-        for b in range(1, IMAGES):
-            nc.sync.dma_start(out=x_raw[b][:], in_=x_rows[b])
-
         b1_f = keep.tile([P, Y_GROUPS, PACK], F32)
-        nc.vector.tensor_copy(out=b1_f[:], in_=b1_bf[:])
         b2_f = keep.tile([P, PACK], F32)
-        nc.vector.tensor_copy(out=b2_f[:], in_=b2_bf[:])
-
+        w1_raw = [keep.tile([P, PACK, K_PASS], BF16, name="w1_raw%d" % g) for g in range(Y_GROUPS)]
+        w2_raw = [keep.tile([P, PACK, C_OUT], BF16, name="w2_raw%d" % g) for g in range(Z_GROUPS)]
+        x_raw = [keep.tile([P, PACK, BLOCK], BF16, name="x_raw%d" % i) for i in range(N_BLOCKS)]
+        w1_grouped = keep.tile([P, Y_GROUPS, PACK, P, PACK], BF16, align_bytes=64)
+        w2_grouped = keep.tile([P, Z_GROUPS, PACK, P, PACK], BF16, align_bytes=64)
         w1_codes = keep.tile([P, Y_GROUPS, K_PASS], U32, align_bytes=64)
         w1_scales = keep.tile([P, Y_GROUPS, K_PASS], U8, align_bytes=64)
         w2_codes = keep.tile([P, Z_GROUPS, C_OUT], U32, align_bytes=64)
         w2_scales = keep.tile([P, Z_GROUPS, C_OUT], U8, align_bytes=64)
 
+        x_grouped, x_codes, x_scales = {}, {}, {}
+        z, z_codes, z_scales, planes = {}, {}, {}, {}
+        y_bank, acc = {}, {}
+
+        def live(block):
+            return 0 <= block < N_BLOCKS
+
+        def load_x(block):
+            b, part = divmod(block, BLOCKS_PER_IMAGE)
+            cols = slice(part * BLOCK, (part + 1) * BLOCK)
+            nc.sync.dma_start(out=x_raw[block][:], in_=x_rows[b][:, :, cols])
+
+        def load_w1(g):
+            nc.sync.dma_start(out=w1_raw[g][:], in_=w1_rows[:, :, g * K_PASS : (g + 1) * K_PASS])
+
+        def load_w2(g):
+            nc.sync.dma_start(out=w2_raw[g][:], in_=w2_rows[g])
+
+        def regroup_x(copy, block, half):
+            if not live(block):
+                return
+            if half == 0:
+                x_grouped[block] = xstage.tile([P, BLOCK, PACK], BF16, align_bytes=64, name="x_grouped")
+            cols = slice(half * HALF, (half + 1) * HALF)
+            regroup_pixels(copy, x_grouped[block][:, cols, :], x_raw[block][:, :, cols])
+
         def quantise_x(block):
-            b, half = divmod(block, BLOCKS_PER_IMAGE)
-            cols = slice(half * BLOCK, (half + 1) * BLOCK)
-            x_grouped = xstage.tile([P, BLOCK, PACK], BF16, align_bytes=64)
-            regroup_pixels(nc.scalar.copy, x_grouped[:], x_raw[b][:, :, cols])
-            x_codes = xstage.tile([P, BLOCK], U32, align_bytes=64)
-            x_scales = xstage.tile([P, BLOCK], U8, align_bytes=64)
+            if not live(block):
+                return
+            x_codes[block] = xstage.tile([P, BLOCK], U32, align_bytes=64, name="x_codes")
+            x_scales[block] = xstage.tile([P, BLOCK], U8, align_bytes=64, name="x_scales")
             nc.vector.quantize_mx(
-                out=x_codes[:].bitcast(FP8X4),
-                scales=x_scales[:],
-                in_=x_grouped[:].rearrange("p n t -> p (n t)"),
+                out=x_codes[block][:].bitcast(FP8X4),
+                scales=x_scales[block][:],
+                in_=x_grouped[block][:].rearrange("p n t -> p (n t)"),
             )
-            return x_codes, x_scales
 
-        def quantise_weight(copy, rows, codes, scales):
-            w_grouped = wstage.tile([P, PACK, P, PACK], BF16, align_bytes=64)
-            regroup_weight(copy, w_grouped[:], rows)
+        def regroup_w1(copy, g):
+            regroup_weight(copy, w1_grouped[:, g], w1_raw[g][:])
+
+        def regroup_w2(copy, g):
+            regroup_weight(copy, w2_grouped[:, g], w2_raw[g][:])
+
+        def quantise_weight(grouped, codes, scales, g):
             nc.vector.quantize_mx(
-                out=codes.bitcast(FP8X4),
-                scales=scales,
-                in_=w_grouped[:].rearrange("p a q t -> p (a q t)"),
+                out=codes[:, g, :].bitcast(FP8X4),
+                scales=scales[:, g, :],
+                in_=grouped[:, g].rearrange("p a q t -> p (a q t)"),
             )
 
-        next_x = quantise_x(0)
-        for g in range(Y_GROUPS):
-            quantise_weight(
-                nc.vector.tensor_copy,
-                w1_raw[:, :, g * K_PASS : (g + 1) * K_PASS],
-                w1_codes[:, g, :],
-                w1_scales[:, g, :],
+        def hidden_pass(y_part, block, g, a, cols):
+            w_cols = slice(a * P, (a + 1) * P)
+            nc.tensor.matmul_mx(
+                out=y_part,
+                lhsT=w1_codes[:, g, w_cols].bitcast(FP8X4),
+                lhsT_scale=w1_scales[:, g, w_cols],
+                rhs=x_codes[block][:, cols].bitcast(FP8X4),
+                rhs_scale=x_scales[block][:, cols],
+                start=True,
+                stop=True,
             )
 
-        for block in range(IMAGES * BLOCKS_PER_IMAGE):
-            b, half = divmod(block, BLOCKS_PER_IMAGE)
-            x_codes, x_scales = next_x
-            if block + 1 < IMAGES * BLOCKS_PER_IMAGE:
-                next_x = quantise_x(block + 1)
-            if block == 0:
-                for g in range(Z_GROUPS):
-                    quantise_weight(nc.scalar.copy, w2_raw[:, g], w2_codes[:, g, :], w2_scales[:, g, :])
+        def hidden_quad(block, g, quad):
+            if not live(block):
+                return
+            y = y_psum.tile([P, PACK, QUAD], F32, name="y_quad", tag="y")
+            y_bank[(block, g, quad)] = y
+            for a in range(PACK):
+                hidden_pass(y[:, a, :], block, g, a, slice(quad * QUAD, (quad + 1) * QUAD))
 
-            z = zstage.tile([P, Z_GROUPS, BLOCK, PACK], BF16, align_bytes=64)
-            z_codes = zstage.tile([P, Z_GROUPS, BLOCK], U32, align_bytes=64)
-            z_scales = zstage.tile([P, Z_GROUPS, BLOCK], U8, align_bytes=64)
+        def z_tiles(block):
+            if block not in z:
+                z[block] = zstage.tile([P, Z_GROUPS, BLOCK, PACK], BF16, align_bytes=64, name="z")
+                z_codes[block] = zstage.tile([P, Z_GROUPS, BLOCK], U32, align_bytes=64, name="z_codes")
+                z_scales[block] = zstage.tile([P, Z_GROUPS, BLOCK], U8, align_bytes=64, name="z_scales")
+            return z[block]
 
-            def quantise_z(g):
-                nc.vector.quantize_mx(
-                    out=z_codes[:, g, :].bitcast(FP8X4),
-                    scales=z_scales[:, g, :],
-                    in_=z[:, g].rearrange("p n t -> p (n t)"),
+        def drain_quad(block, g, quad):
+            if not live(block):
+                return
+            nc.vector.tensor_tensor(
+                out=z_tiles(block)[:, g, quad * QUAD : (quad + 1) * QUAD, :],
+                in0=y_bank[(block, g, quad)][:].rearrange("p a n -> p n a"),
+                in1=b1_f[:, g, :].unsqueeze(1).to_broadcast([P, QUAD, PACK]),
+                op=ADD,
+            )
+
+        def hidden_pair(block, pair):
+            if not live(block):
+                return
+            y = y_psum.tile([P, 2, HALF], F32, name="y_pair", tag="y")
+            y_bank[(block, A, "pair", pair)] = y
+            for i in range(2):
+                hidden_pass(y[:, i, :], block, A, 2 * pair + i, slice(0, HALF))
+
+        def drain_pair(block, pair):
+            if not live(block):
+                return
+            if pair == 0:
+                planes[block] = zstage.tile([P, PACK, HALF], BF16, name="planes")
+            for i in range(2):
+                a = 2 * pair + i
+                nc.scalar.activation(
+                    out=planes[block][:, a, :],
+                    in_=y_bank[(block, A, "pair", pair)][:, i, :],
+                    func=IDENTITY,
+                    bias=b1_f[:, A, a : a + 1],
+                    scale=1.0,
                 )
 
-            for g in range(Y_GROUPS):
-                for quad in range(PACK):
-                    cols = slice(quad * QUAD, (quad + 1) * QUAD)
-                    y = y_psum.tile([P, PACK, QUAD], F32)
-                    for a in range(PACK):
-                        w_cols = slice(a * P, (a + 1) * P)
-                        nc.tensor.matmul_mx(
-                            out=y[:, a, :],
-                            lhsT=w1_codes[:, g, w_cols].bitcast(FP8X4),
-                            lhsT_scale=w1_scales[:, g, w_cols],
-                            rhs=x_codes[:, cols].bitcast(FP8X4),
-                            rhs_scale=x_scales[:, cols],
-                            start=True,
-                            stop=True,
-                        )
-                    nc.vector.tensor_tensor(
-                        out=z[:, g, cols, :],
-                        in0=y[:].rearrange("p a n -> p n a"),
-                        in1=b1_f[:, g, :].unsqueeze(1).to_broadcast([P, QUAD, PACK]),
-                        op=ADD,
-                    )
-                quantise_z(g)
+        def regroup_planes(block):
+            if not live(block):
+                return
+            regroup_pixels(nc.vector.tensor_copy, z_tiles(block)[:, A, 0:HALF, :], planes[block][:])
+
+        def relu(block):
+            if not live(block):
+                return
             nc.vector.tensor_scalar_max(
-                out=z[:, 2].rearrange("p n t -> p (n t)"),
-                in0=z[:, 1].rearrange("p n t -> p (n t)"),
+                out=z[block][:, RELU].rearrange("p n t -> p (n t)"),
+                in0=z[block][:, FMAP].rearrange("p n t -> p (n t)"),
                 scalar1=0.0,
             )
-            quantise_z(2)
 
-            acc = [o_psum.tile([P, BLOCK], F32, name="acc%d" % m) for m in range(PACK)]
-            for g in range(Z_GROUPS):
-                for m in range(PACK):
-                    w_cols = slice(m * P, (m + 1) * P)
-                    nc.tensor.matmul_mx(
-                        out=acc[m][:],
-                        lhsT=w2_codes[:, g, w_cols].bitcast(FP8X4),
-                        lhsT_scale=w2_scales[:, g, w_cols],
-                        rhs=z_codes[:, g, :].bitcast(FP8X4),
-                        rhs_scale=z_scales[:, g, :],
-                        start=(g == 0),
-                        stop=(g == Z_GROUPS - 1),
-                    )
-            result = ostage.tile([P, PACK, BLOCK], F32)
-            for m in range(PACK):
-                nc.scalar.activation(
-                    out=result[:, m, :], in_=acc[m][:], func=IDENTITY, bias=b2_f[:, m : m + 1], scale=1.0
-                )
-            nc.sync.dma_start(
-                out=out_rows[b][:, :, half * BLOCK : (half + 1) * BLOCK], in_=result[:]
+        def quantise_z(block, g):
+            if not live(block):
+                return
+            nc.vector.quantize_mx(
+                out=z_codes[block][:, g, :].bitcast(FP8X4),
+                scales=z_scales[block][:, g, :],
+                in_=z[block][:, g].rearrange("p n t -> p (n t)"),
             )
+
+        def output_passes(block, g):
+            if not live(block):
+                return
+            if g == 0:
+                acc[block] = [o_psum.tile([P, BLOCK], F32, name="acc%d" % m) for m in range(PACK)]
+            for m in range(PACK):
+                w_cols = slice(m * P, (m + 1) * P)
+                nc.tensor.matmul_mx(
+                    out=acc[block][m][:],
+                    lhsT=w2_codes[:, g, w_cols].bitcast(FP8X4),
+                    lhsT_scale=w2_scales[:, g, w_cols],
+                    rhs=z_codes[block][:, g, :].bitcast(FP8X4),
+                    rhs_scale=z_scales[block][:, g, :],
+                    start=(g == 0),
+                    stop=(g == Z_GROUPS - 1),
+                )
+
+        def drain_output(block):
+            if not live(block):
+                return
+            b, part = divmod(block, BLOCKS_PER_IMAGE)
+            for m in range(PACK):
+                result = ostage.tile([P, BLOCK], F32, name="result")
+                if block == N_BLOCKS - 1 and m % 2 == 1:
+                    nc.vector.tensor_scalar_add(
+                        out=result[:], in0=acc[block][m][:], scalar1=b2_f[:, m : m + 1]
+                    )
+                else:
+                    nc.scalar.activation(
+                        out=result[:], in_=acc[block][m][:], func=IDENTITY, bias=b2_f[:, m : m + 1], scale=1.0
+                    )
+                nc.sync.dma_start(out=out_rows[b][:, m, part * BLOCK : (part + 1) * BLOCK], in_=result[:])
+
+        load_x(0)
+        load_w1(A)
+        load_w1(FMAP)
+        nc.sync.dma_start(out=b1_bf[:], in_=b1.rearrange("(g p a) -> p g a", g=Y_GROUPS, a=PACK))
+        load_w2(RELU)
+        load_x(1)
+        load_w2(A)
+        load_w2(FMAP)
+        nc.sync.dma_start(out=b2_bf[:], in_=b2.rearrange("(p m) -> p m", m=PACK))
+        for block in range(2, N_BLOCKS):
+            load_x(block)
+
+        regroup_x(nc.vector.tensor_copy, 0, 0)
+        regroup_x(nc.vector.tensor_copy, 0, 1)
+        regroup_w1(nc.vector.tensor_copy, A)
+        regroup_w1(nc.scalar.copy, FMAP)
+        regroup_w2(nc.scalar.copy, RELU)
+        quantise_x(0)
+        quantise_weight(w1_grouped, w1_codes, w1_scales, A)
+        nc.vector.tensor_copy(out=b1_f[:], in_=b1_bf[:])
+        quantise_weight(w1_grouped, w1_codes, w1_scales, FMAP)
+        regroup_w2(nc.vector.tensor_copy, A)
+        regroup_w2(nc.vector.tensor_copy, FMAP)
+        quantise_weight(w2_grouped, w2_codes, w2_scales, A)
+        quantise_weight(w2_grouped, w2_codes, w2_scales, FMAP)
+        nc.vector.tensor_copy(out=b2_f[:], in_=b2_bf[:])
+        quantise_weight(w2_grouped, w2_codes, w2_scales, RELU)
+
+        for i in range(-1, N_BLOCKS + 1):
+            drain_output(i - 1)
+            drain_quad(i, FMAP, 0)
+            quantise_z(i, A)
+            hidden_quad(i + 1, A, 2)
+            output_passes(i, A)
+            for quad in range(1, PACK):
+                drain_quad(i, FMAP, quad)
+            hidden_quad(i + 1, A, 3)
+            regroup_x(nc.scalar.copy, i + 2, 0)
+            for pair in range(2):
+                hidden_pair(i + 1, pair)
+                drain_pair(i + 1, pair)
+            regroup_x(nc.scalar.copy, i + 2, 1)
+            drain_quad(i + 1, A, 2)
+            relu(i)
+            quantise_z(i, FMAP)
+            for quad in range(3):
+                hidden_quad(i + 1, FMAP, quad)
+            output_passes(i, FMAP)
+            drain_quad(i + 1, A, 3)
+            hidden_quad(i + 1, FMAP, 3)
+            quantise_z(i, RELU)
+            output_passes(i, RELU)
+            regroup_planes(i + 1)
+            quantise_x(i + 2)

@@ -8,6 +8,7 @@ U32 = mybir.dt.uint32
 U8 = mybir.dt.uint8
 FP8X4 = mybir.dt.float8_e4m3fn_x4
 ADD = mybir.AluOpType.add
+MULT = mybir.AluOpType.mult
 IDENTITY = mybir.ActivationFunctionType.Identity
 
 P = 128
@@ -185,10 +186,15 @@ def tile_offm_pa_t_kernel(tc, x, w1, b1, w2, b2, out):
                     scale=1.0,
                 )
 
+        def gpsimd_copy(out, in_):
+            nc.gpsimd.tensor_scalar(out=out, in0=in_, scalar1=1.0, scalar2=0.0, op0=MULT, op1=ADD)
+
         def regroup_planes(block):
             if not live(block):
                 return
-            regroup_pixels(nc.vector.tensor_copy, z_tiles(block)[:, A, 0:HALF, :], planes[block][:])
+            for quad in range(HALF // QUAD):
+                cols = slice(quad * QUAD, (quad + 1) * QUAD)
+                regroup_pixels(gpsimd_copy, z_tiles(block)[:, A, cols, :], planes[block][:, :, cols])
 
         def relu(block):
             if not live(block):

@@ -8,7 +8,6 @@ U32 = mybir.dt.uint32
 U8 = mybir.dt.uint8
 FP8X4 = mybir.dt.float8_e4m3fn_x4
 ADD = mybir.AluOpType.add
-MULT = mybir.AluOpType.mult
 IDENTITY = mybir.ActivationFunctionType.Identity
 
 P = 128
@@ -55,7 +54,6 @@ def tile_offm_pa_t_kernel(tc, x, w1, b1, w2, b2, out):
         ostage = ctx.enter_context(tc.tile_pool(name="ostage", bufs=8))
         y_psum = ctx.enter_context(tc.psum_pool(name="y_psum", bufs=4))
         o_psum = ctx.enter_context(tc.psum_pool(name="o_psum", bufs=1))
-        ctx.enter_context(tc.manual_schedule())
 
         x_rows = x.rearrange("b (p t) h w -> b p t (h w)", t=PACK)
         w1_rows = w1.rearrange("(p t) d -> p t d", t=PACK)
@@ -186,15 +184,11 @@ def tile_offm_pa_t_kernel(tc, x, w1, b1, w2, b2, out):
                     scale=1.0,
                 )
 
-        def gpsimd_copy(out, in_):
-            nc.gpsimd.tensor_scalar(out=out, in0=in_, scalar1=1.0, scalar2=0.0, op0=MULT, op1=ADD)
-
-        def regroup_planes(block):
+        def regroup_planes(copy, block, quad):
             if not live(block):
                 return
-            for quad in range(HALF // QUAD):
-                cols = slice(quad * QUAD, (quad + 1) * QUAD)
-                regroup_pixels(gpsimd_copy, z_tiles(block)[:, A, cols, :], planes[block][:, :, cols])
+            cols = slice(quad * QUAD, (quad + 1) * QUAD)
+            regroup_pixels(copy, z_tiles(block)[:, A, cols, :], planes[block][:, :, cols])
 
         def relu(block):
             if not live(block):
@@ -269,7 +263,7 @@ def tile_offm_pa_t_kernel(tc, x, w1, b1, w2, b2, out):
         nc.vector.tensor_copy(out=b1_f[:], in_=b1_bf[:])
         quantise_weight(w1_grouped, w1_codes, w1_scales, FMAP)
         regroup_w2(nc.vector.tensor_copy, A)
-        regroup_w2(nc.vector.tensor_copy, FMAP)
+        regroup_w2(nc.scalar.copy, FMAP)
         quantise_weight(w2_grouped, w2_codes, w2_scales, A)
         quantise_weight(w2_grouped, w2_codes, w2_scales, FMAP)
         nc.vector.tensor_copy(out=b2_f[:], in_=b2_bf[:])
@@ -290,6 +284,7 @@ def tile_offm_pa_t_kernel(tc, x, w1, b1, w2, b2, out):
                 drain_pair(i + 1, pair)
             regroup_x(nc.scalar.copy, i + 2, 1)
             drain_quad(i + 1, A, 2)
+            regroup_planes(nc.scalar.copy, i + 1, 0)
             relu(i)
             quantise_z(i, FMAP)
             for quad in range(3):
@@ -299,5 +294,5 @@ def tile_offm_pa_t_kernel(tc, x, w1, b1, w2, b2, out):
             hidden_quad(i + 1, FMAP, 3)
             quantise_z(i, RELU)
             output_passes(i, RELU)
-            regroup_planes(i + 1)
+            regroup_planes(nc.scalar.copy, i + 1, 1)
             quantise_x(i + 2)

@@ -231,39 +231,32 @@ def tile_offm_pa_t_kernel(tc, x, w1, b1, w2, b2, out):
             b, part = divmod(block, BLOCKS_PER_IMAGE)
             for m in range(PACK):
                 result = ostage.tile([P, BLOCK], F32, name="result")
-                if block == N_BLOCKS - 1 and m % 2 == 1:
-                    nc.vector.tensor_scalar_add(
-                        out=result[:], in0=acc[block][m][:], scalar1=b2_f[:, m : m + 1]
-                    )
-                else:
-                    nc.scalar.activation(
-                        out=result[:], in_=acc[block][m][:], func=IDENTITY, bias=b2_f[:, m : m + 1], scale=1.0
-                    )
+                nc.any.tensor_scalar_add(out=result[:], in0=acc[block][m][:], scalar1=b2_f[:, m : m + 1])
                 nc.sync.dma_start(out=out_rows[b][:, m, part * BLOCK : (part + 1) * BLOCK], in_=result[:])
 
         load_x(0)
         load_w1(A)
         load_w1(FMAP)
         nc.sync.dma_start(out=b1_bf[:], in_=b1.rearrange("(g p a) -> p g a", g=Y_GROUPS, a=PACK))
-        load_w2(RELU)
         load_x(1)
         load_w2(A)
         load_w2(FMAP)
+        load_w2(RELU)
         nc.sync.dma_start(out=b2_bf[:], in_=b2.rearrange("(p m) -> p m", m=PACK))
         for block in range(2, N_BLOCKS):
             load_x(block)
 
-        regroup_x(nc.vector.tensor_copy, 0, 0)
-        regroup_x(nc.vector.tensor_copy, 0, 1)
-        regroup_w1(nc.vector.tensor_copy, A)
-        regroup_w1(nc.scalar.copy, FMAP)
-        regroup_w2(nc.scalar.copy, RELU)
+        regroup_x(nc.any.tensor_copy, 0, 0)
+        regroup_x(nc.any.tensor_copy, 0, 1)
+        regroup_w1(nc.any.tensor_copy, A)
+        regroup_w1(nc.any.tensor_copy, FMAP)
         quantise_x(0)
         quantise_weight(w1_grouped, w1_codes, w1_scales, A)
         nc.vector.tensor_copy(out=b1_f[:], in_=b1_bf[:])
         quantise_weight(w1_grouped, w1_codes, w1_scales, FMAP)
-        regroup_w2(nc.vector.tensor_copy, A)
-        regroup_w2(nc.scalar.copy, FMAP)
+        regroup_w2(nc.any.tensor_copy, A)
+        regroup_w2(nc.any.tensor_copy, FMAP)
+        regroup_w2(nc.any.tensor_copy, RELU)
         quantise_weight(w2_grouped, w2_codes, w2_scales, A)
         quantise_weight(w2_grouped, w2_codes, w2_scales, FMAP)
         nc.vector.tensor_copy(out=b2_f[:], in_=b2_bf[:])
@@ -278,13 +271,13 @@ def tile_offm_pa_t_kernel(tc, x, w1, b1, w2, b2, out):
             for quad in range(1, PACK):
                 drain_quad(i, FMAP, quad)
             hidden_quad(i + 1, A, 3)
-            regroup_x(nc.scalar.copy, i + 2, 0)
+            regroup_x(nc.any.tensor_copy, i + 2, 0)
             for pair in range(2):
                 hidden_pair(i + 1, pair)
                 drain_pair(i + 1, pair)
-            regroup_x(nc.scalar.copy, i + 2, 1)
+            regroup_x(nc.any.tensor_copy, i + 2, 1)
             drain_quad(i + 1, A, 2)
-            regroup_planes(nc.scalar.copy, i + 1, 0)
+            regroup_planes(nc.any.tensor_copy, i + 1, 0)
             relu(i)
             quantise_z(i, FMAP)
             for quad in range(3):
@@ -294,5 +287,5 @@ def tile_offm_pa_t_kernel(tc, x, w1, b1, w2, b2, out):
             hidden_quad(i + 1, FMAP, 3)
             quantise_z(i, RELU)
             output_passes(i, RELU)
-            regroup_planes(nc.scalar.copy, i + 1, 1)
+            regroup_planes(nc.any.tensor_copy, i + 1, 1)
             quantise_x(i + 2)

@@ -1,6 +1,7 @@
 from contextlib import ExitStack
 
 import concourse.mybir as mybir
+from concourse.masks import make_identity
 
 BF16 = mybir.dt.bfloat16
 F32 = mybir.dt.float32
@@ -8,6 +9,7 @@ U32 = mybir.dt.uint32
 U8 = mybir.dt.uint8
 FP8X4 = mybir.dt.float8_e4m3fn_x4
 ADD = mybir.AluOpType.add
+MULT = mybir.AluOpType.mult
 IDENTITY = mybir.ActivationFunctionType.Identity
 
 P = 128
@@ -38,10 +40,10 @@ def regroup_pixels(copy, grouped, rows):
     )
 
 
-def regroup_weight(copy, grouped, rows):
+def regroup_weight(copy, grouped, rows, q0=0, q1=P):
     copy(
-        out=grouped.rearrange("p a q t -> p q t a"),
-        in_=rows.rearrange("p t (q a) -> p q t a", a=PACK),
+        out=grouped[:, :, q0:q1, :].rearrange("p a q t -> p q t a"),
+        in_=rows[:, :, PACK * q0 : PACK * q1].rearrange("p t (q a) -> p q t a", a=PACK),
     )
 
 
@@ -49,11 +51,12 @@ def tile_offm_pa_t_kernel(tc, x, w1, b1, w2, b2, out):
     nc = tc.nc
     with ExitStack() as ctx:
         keep = ctx.enter_context(tc.tile_pool(name="keep", bufs=1))
+        xg = ctx.enter_context(tc.tile_pool(name="xg", bufs=1))
         xstage = ctx.enter_context(tc.tile_pool(name="xstage", bufs=2))
-        zstage = ctx.enter_context(tc.tile_pool(name="zstage", bufs=2))
+        zstage = ctx.enter_context(tc.tile_pool(name="zstage", bufs=3))
         ostage = ctx.enter_context(tc.tile_pool(name="ostage", bufs=8))
-        y_psum = ctx.enter_context(tc.psum_pool(name="y_psum", bufs=4))
-        o_psum = ctx.enter_context(tc.psum_pool(name="o_psum", bufs=1))
+        y_psum = ctx.enter_context(tc.psum_pool(name="y_psum", bufs=5))
+        o_psum = ctx.enter_context(tc.psum_pool(name="o_psum", bufs=3))
 
         x_rows = x.rearrange("b (p t) h w -> b p t (h w)", t=PACK)
         w1_rows = w1.rearrange("(p t) d -> p t d", t=PACK)
@@ -62,8 +65,6 @@ def tile_offm_pa_t_kernel(tc, x, w1, b1, w2, b2, out):
 
         b1_bf = keep.tile([P, Y_GROUPS, PACK], BF16)
         b2_bf = keep.tile([P, PACK], BF16)
-        b1_f = keep.tile([P, Y_GROUPS, PACK], F32)
-        b2_f = keep.tile([P, PACK], F32)
         w1_raw = [keep.tile([P, PACK, K_PASS], BF16, name="w1_raw%d" % g) for g in range(Y_GROUPS)]
         w2_raw = [keep.tile([P, PACK, C_OUT], BF16, name="w2_raw%d" % g) for g in range(Z_GROUPS)]
         x_raw = [keep.tile([P, PACK, BLOCK], BF16, name="x_raw%d" % i) for i in range(N_BLOCKS)]
@@ -76,7 +77,9 @@ def tile_offm_pa_t_kernel(tc, x, w1, b1, w2, b2, out):
 
         x_grouped, x_codes, x_scales = {}, {}, {}
         z, z_codes, z_scales, planes = {}, {}, {}, {}
-        y_bank, acc = {}, {}
+        y_bank, acc, w_bank = {}, {}, {}
+        ident = keep.tile([P, P], BF16, name="ident")
+        make_identity(nc, ident[:])
 
         def live(block):
             return 0 <= block < N_BLOCKS
@@ -92,12 +95,12 @@ def tile_offm_pa_t_kernel(tc, x, w1, b1, w2, b2, out):
         def load_w2(g):
             nc.sync.dma_start(out=w2_raw[g][:], in_=w2_rows[g])
 
-        def regroup_x(copy, block, half):
+        def regroup_x(copy, block, first, last):
             if not live(block):
                 return
-            if half == 0:
-                x_grouped[block] = xstage.tile([P, BLOCK, PACK], BF16, align_bytes=64, name="x_grouped")
-            cols = slice(half * HALF, (half + 1) * HALF)
+            if block not in x_grouped:
+                x_grouped[block] = xg.tile([P, BLOCK, PACK], BF16, align_bytes=64, name="x_grouped")
+            cols = slice(first * QUAD, last * QUAD)
             regroup_pixels(copy, x_grouped[block][:, cols, :], x_raw[block][:, :, cols])
 
         def quantise_x(block):
@@ -111,11 +114,27 @@ def tile_offm_pa_t_kernel(tc, x, w1, b1, w2, b2, out):
                 in_=x_grouped[block][:].rearrange("p n t -> p (n t)"),
             )
 
-        def regroup_w1(copy, g):
-            regroup_weight(copy, w1_grouped[:, g], w1_raw[g][:])
+        def regroup_w(copy, grouped, raw, g, q0, q1):
+            regroup_weight(copy, grouped[:, g], raw[g][:], q0, q1)
 
-        def regroup_w2(copy, g):
-            regroup_weight(copy, w2_grouped[:, g], w2_raw[g][:])
+        def interleave_w2(g, half):
+            bank = o_psum.tile([P, 2, P, PACK], BF16, name="w2_bank", tag="acc")
+            w_bank[(g, half)] = bank
+            columns = w2_raw[g][:].rearrange("p t (q a) -> p a q t", a=PACK)
+            for i in range(2):
+                nc.tensor.matmul(
+                    bank[:, i].rearrange("p q t -> p (q t)"),
+                    ident[:],
+                    columns[:, 2 * half + i],
+                    start=True,
+                    stop=True,
+                )
+
+        def empty_w2(copy, g, half):
+            copy(
+                out=w2_grouped[:, g, 2 * half : 2 * half + 2].rearrange("p a q t -> p (a q t)"),
+                in_=w_bank[(g, half)][:].rearrange("p a q t -> p (a q t)"),
+            )
 
         def quantise_weight(grouped, codes, scales, g):
             nc.vector.quantize_mx(
@@ -157,7 +176,7 @@ def tile_offm_pa_t_kernel(tc, x, w1, b1, w2, b2, out):
             nc.vector.tensor_tensor(
                 out=z_tiles(block)[:, g, quad * QUAD : (quad + 1) * QUAD, :],
                 in0=y_bank[(block, g, quad)][:].rearrange("p a n -> p n a"),
-                in1=b1_f[:, g, :].unsqueeze(1).to_broadcast([P, QUAD, PACK]),
+                in1=b1_bf[:, g, :].unsqueeze(1).to_broadcast([P, QUAD, PACK]),
                 op=ADD,
             )
 
@@ -173,14 +192,26 @@ def tile_offm_pa_t_kernel(tc, x, w1, b1, w2, b2, out):
             if not live(block):
                 return
             if pair == 0:
-                planes[block] = zstage.tile([P, PACK, HALF], BF16, name="planes")
+                planes[block] = zstage.tile([P, PACK, BLOCK], BF16, name="planes")
             for i in range(2):
                 a = 2 * pair + i
                 nc.scalar.activation(
-                    out=planes[block][:, a, :],
+                    out=planes[block][:, a, 0:HALF],
                     in_=y_bank[(block, A, "pair", pair)][:, i, :],
                     func=IDENTITY,
-                    bias=b1_f[:, A, a : a + 1],
+                    bias=b1_bf[:, A, a : a + 1],
+                    scale=1.0,
+                )
+
+        def drain_quad_planes(block, quad):
+            if not live(block):
+                return
+            for a in range(PACK):
+                nc.scalar.activation(
+                    out=planes[block][:, a, quad * QUAD : (quad + 1) * QUAD],
+                    in_=y_bank[(block, A, quad)][:, a, :],
+                    func=IDENTITY,
+                    bias=b1_bf[:, A, a : a + 1],
                     scale=1.0,
                 )
 
@@ -208,31 +239,65 @@ def tile_offm_pa_t_kernel(tc, x, w1, b1, w2, b2, out):
                 in_=z[block][:, g].rearrange("p n t -> p (n t)"),
             )
 
-        def output_passes(block, g):
+        def output_pass(block, g, m):
+            w_cols = slice(m * P, (m + 1) * P)
+            nc.tensor.matmul_mx(
+                out=acc[(block, m)][:],
+                lhsT=w2_codes[:, g, w_cols].bitcast(FP8X4),
+                lhsT_scale=w2_scales[:, g, w_cols],
+                rhs=z_codes[block][:, g, :].bitcast(FP8X4),
+                rhs_scale=z_scales[block][:, g, :],
+                start=(g == 0),
+                stop=(g == Z_GROUPS - 1),
+            )
+
+        def output_bank(block, m):
             if not live(block):
                 return
-            if g == 0:
-                acc[block] = [o_psum.tile([P, BLOCK], F32, name="acc%d" % m) for m in range(PACK)]
-            for m in range(PACK):
-                w_cols = slice(m * P, (m + 1) * P)
-                nc.tensor.matmul_mx(
-                    out=acc[block][m][:],
-                    lhsT=w2_codes[:, g, w_cols].bitcast(FP8X4),
-                    lhsT_scale=w2_scales[:, g, w_cols],
-                    rhs=z_codes[block][:, g, :].bitcast(FP8X4),
-                    rhs_scale=z_scales[block][:, g, :],
-                    start=(g == 0),
-                    stop=(g == Z_GROUPS - 1),
-                )
+            acc[(block, m)] = o_psum.tile([P, BLOCK], F32, name="acc")
+            for g in range(Z_GROUPS):
+                output_pass(block, g, m)
 
-        def drain_output(block):
+        def output_group_last(g):
+            for m in range(PACK):
+                if g == 0:
+                    acc[(N_BLOCKS - 1, m)] = y_psum.tile([P, BLOCK], F32, name="acc_last", tag="y")
+                output_pass(N_BLOCKS - 1, g, m)
+
+        def drain_output(block, banks, engine):
             if not live(block):
                 return
             b, part = divmod(block, BLOCKS_PER_IMAGE)
-            for m in range(PACK):
+            for m in banks:
                 result = ostage.tile([P, BLOCK], F32, name="result")
-                nc.any.tensor_scalar_add(out=result[:], in0=acc[block][m][:], scalar1=b2_f[:, m : m + 1])
+                if engine == "S":
+                    nc.scalar.activation(
+                        out=result[:], in_=acc[(block, m)][:], func=IDENTITY, bias=b2_bf[:, m : m + 1], scale=1.0
+                    )
+                else:
+                    nc.vector.tensor_scalar_add(out=result[:], in0=acc[(block, m)][:], scalar1=b2_bf[:, m : m + 1])
                 nc.sync.dma_start(out=out_rows[b][:, m, part * BLOCK : (part + 1) * BLOCK], in_=result[:])
+
+        def regroup_x_gp(block, first, last):
+            if not live(block):
+                return
+            if block not in x_grouped:
+                x_grouped[block] = xg.tile([P, BLOCK, PACK], BF16, align_bytes=64, name="x_grouped")
+            cols = slice(first, last)
+            gp_copy(x_grouped[block][:, cols, :], x_raw[block][:, :, cols].rearrange("p t n -> p n t"))
+
+        def regroup_x_s(block, first, last):
+            if not live(block):
+                return
+            if block not in x_grouped:
+                x_grouped[block] = xg.tile([P, BLOCK, PACK], BF16, align_bytes=64, name="x_grouped")
+            cols = slice(first, last)
+            regroup_pixels(nc.scalar.copy, x_grouped[block][:, cols, :], x_raw[block][:, :, cols])
+
+        def gp_copy(out, in_):
+            nc.gpsimd.tensor_scalar(out=out, in0=in_, scalar1=1.0, scalar2=0.0, op0=MULT, op1=ADD)
+
+        V, S = nc.vector.tensor_copy, nc.scalar.copy
 
         load_x(0)
         load_w1(A)
@@ -246,46 +311,133 @@ def tile_offm_pa_t_kernel(tc, x, w1, b1, w2, b2, out):
         for block in range(2, N_BLOCKS):
             load_x(block)
 
-        regroup_x(nc.any.tensor_copy, 0, 0)
-        regroup_x(nc.any.tensor_copy, 0, 1)
-        regroup_w1(nc.any.tensor_copy, A)
-        regroup_w1(nc.any.tensor_copy, FMAP)
-        quantise_x(0)
-        quantise_weight(w1_grouped, w1_codes, w1_scales, A)
-        nc.vector.tensor_copy(out=b1_f[:], in_=b1_bf[:])
-        quantise_weight(w1_grouped, w1_codes, w1_scales, FMAP)
-        regroup_w2(nc.any.tensor_copy, A)
-        regroup_w2(nc.any.tensor_copy, FMAP)
-        regroup_w2(nc.any.tensor_copy, RELU)
-        quantise_weight(w2_grouped, w2_codes, w2_scales, A)
-        quantise_weight(w2_grouped, w2_codes, w2_scales, FMAP)
-        nc.vector.tensor_copy(out=b2_f[:], in_=b2_bf[:])
-        quantise_weight(w2_grouped, w2_codes, w2_scales, RELU)
+        def gpsimd_x(block):
+            for first in (64, 192, 320, 448):
+                regroup_x_gp(block, first, min(first + 128, BLOCK))
 
-        for i in range(-1, N_BLOCKS + 1):
-            drain_output(i - 1)
+        def round_(i):
+            if i + 2 < N_BLOCKS:
+                gpsimd_x(i + 2)
+            regroup_planes(S, i, 0)
             drain_quad(i, FMAP, 0)
-            quantise_z(i, A)
-            hidden_quad(i + 1, A, 2)
-            output_passes(i, A)
-            for quad in range(1, PACK):
-                drain_quad(i, FMAP, quad)
+            output_bank(i - 1, 0)
             hidden_quad(i + 1, A, 3)
-            regroup_x(nc.any.tensor_copy, i + 2, 0)
-            for pair in range(2):
-                hidden_pair(i + 1, pair)
-                drain_pair(i + 1, pair)
-            regroup_x(nc.any.tensor_copy, i + 2, 1)
-            drain_quad(i + 1, A, 2)
-            regroup_planes(nc.any.tensor_copy, i + 1, 0)
-            relu(i)
-            quantise_z(i, FMAP)
-            for quad in range(3):
-                hidden_quad(i + 1, FMAP, quad)
-            output_passes(i, FMAP)
+            drain_quad(i, FMAP, 1)
+            hidden_pair(i + 1, 0)
+            drain_output(i - 1, [0], "S")
+            drain_pair(i + 1, 0)
+            drain_quad(i, FMAP, 2)
+            output_bank(i - 1, 1)
+            hidden_pair(i + 1, 1)
+            regroup_planes(S, i, 1)
+            drain_output(i - 1, [1], "S")
+            drain_quad(i, FMAP, 3)
+            hidden_quad(i + 1, A, 2)
+            drain_pair(i + 1, 1)
             drain_quad(i + 1, A, 3)
+            regroup_x_s(i + 2, 0, 64)
+            output_bank(i - 1, 2)
+            hidden_quad(i + 1, FMAP, 0)
+            hidden_quad(i + 1, FMAP, 1)
+            drain_output(i - 1, [2], "S")
+            drain_quad_planes(i + 1, 2)
+            output_bank(i - 1, 3)
+            hidden_quad(i + 1, FMAP, 2)
             hidden_quad(i + 1, FMAP, 3)
-            quantise_z(i, RELU)
-            output_passes(i, RELU)
-            regroup_planes(nc.any.tensor_copy, i + 1, 1)
+            drain_output(i - 1, [3], "S")
+            regroup_planes(V, i, 2)
+            relu(i)
+            for g in range(Z_GROUPS):
+                quantise_z(i, g)
             quantise_x(i + 2)
+
+        with tc.manual_schedule():
+            H = 80
+            regroup_x(V, 0, 0, 3)
+            regroup_x(S, 0, 3, 4)
+            quantise_x(0)
+            regroup_w(S, w1_grouped, w1_raw, A, H, P)
+            regroup_w(V, w1_grouped, w1_raw, A, 0, H)
+            regroup_w(S, w1_grouped, w1_raw, FMAP, H, P)
+            regroup_w(V, w1_grouped, w1_raw, FMAP, 0, H)
+            quantise_weight(w1_grouped, w1_codes, w1_scales, A)
+            quantise_weight(w1_grouped, w1_codes, w1_scales, FMAP)
+            regroup_x(S, 1, 2, 4)
+            regroup_x(V, 1, 0, 2)
+            hidden_quad(0, A, 3)
+            hidden_pair(0, 0)
+            hidden_pair(0, 1)
+            hidden_quad(0, A, 2)
+            drain_quad(0, A, 3)
+            quantise_x(1)
+            interleave_w2(A, 0)
+            interleave_w2(A, 1)
+            drain_pair(0, 0)
+            drain_pair(0, 1)
+            empty_w2(S, A, 0)
+            drain_quad_planes(0, 2)
+            empty_w2(S, A, 1)
+            interleave_w2(FMAP, 0)
+            for quad in range(PACK):
+                hidden_quad(0, FMAP, quad)
+            empty_w2(S, FMAP, 0)
+            gpsimd_x(2)
+            drain_quad(0, FMAP, 0)
+            hidden_quad(1, A, 3)
+            regroup_planes(S, 0, 0)
+            drain_quad(0, FMAP, 1)
+            hidden_pair(1, 0)
+            regroup_planes(S, 0, 1)
+            drain_quad(0, FMAP, 2)
+            hidden_pair(1, 1)
+            drain_quad(0, FMAP, 3)
+            hidden_quad(1, A, 2)
+            interleave_w2(FMAP, 1)
+            interleave_w2(RELU, 0)
+            empty_w2(S, FMAP, 1)
+            interleave_w2(RELU, 1)
+            empty_w2(S, RELU, 0)
+            drain_quad(1, A, 3)
+            empty_w2(S, RELU, 1)
+            drain_pair(1, 0)
+            drain_pair(1, 1)
+            hidden_quad(1, FMAP, 0)
+            hidden_quad(1, FMAP, 1)
+            hidden_quad(1, FMAP, 2)
+            regroup_x_s(2, 0, 64)
+            drain_quad_planes(1, 2)
+            hidden_quad(1, FMAP, 3)
+            regroup_planes(V, 0, 2)
+            relu(0)
+            for g in range(Z_GROUPS):
+                quantise_z(0, g)
+            for g in range(Z_GROUPS):
+                quantise_weight(w2_grouped, w2_codes, w2_scales, g)
+            quantise_x(2)
+            for i in range(1, N_BLOCKS - 1):
+                round_(i)
+            i = N_BLOCKS - 1
+            regroup_planes(S, i, 0)
+            regroup_planes(S, i, 1)
+            regroup_planes(V, i, 2)
+            output_bank(i - 1, 0)
+            drain_quad(i, FMAP, 0)
+            drain_output(i - 1, [0], "S")
+            drain_quad(i, FMAP, 1)
+            output_bank(i - 1, 1)
+            quantise_z(i, A)
+            drain_output(i - 1, [1], "S")
+            drain_quad(i, FMAP, 2)
+            output_bank(i - 1, 2)
+            drain_quad(i, FMAP, 3)
+            drain_output(i - 1, [2], "S")
+            output_bank(i - 1, 3)
+            relu(i)
+            drain_output(i - 1, [3], "S")
+            output_group_last(A)
+            quantise_z(i, FMAP)
+            output_group_last(FMAP)
+            quantise_z(i, RELU)
+            output_group_last(RELU)
+            for m in range(PACK):
+                drain_output(i, [m], "VS"[m % 2])

@@ -1,7 +1,6 @@
 from contextlib import ExitStack
 
 import concourse.mybir as mybir
-from concourse.masks import make_identity
 
 BF16 = mybir.dt.bfloat16
 F32 = mybir.dt.float32
@@ -65,6 +64,8 @@ def tile_offm_pa_t_kernel(tc, x, w1, b1, w2, b2, out):
 
         b1_bf = keep.tile([P, Y_GROUPS, PACK], BF16)
         b2_bf = keep.tile([P, PACK], BF16)
+        b1_f = keep.tile([P, Y_GROUPS, PACK], F32)
+        b2_f = keep.tile([P, PACK], F32)
         w1_raw = [keep.tile([P, PACK, K_PASS], BF16, name="w1_raw%d" % g) for g in range(Y_GROUPS)]
         w2_raw = [keep.tile([P, PACK, C_OUT], BF16, name="w2_raw%d" % g) for g in range(Z_GROUPS)]
         x_raw = [keep.tile([P, PACK, BLOCK], BF16, name="x_raw%d" % i) for i in range(N_BLOCKS)]
@@ -77,9 +78,7 @@ def tile_offm_pa_t_kernel(tc, x, w1, b1, w2, b2, out):
 
         x_grouped, x_codes, x_scales = {}, {}, {}
         z, z_codes, z_scales, planes = {}, {}, {}, {}
-        y_bank, acc, w_bank = {}, {}, {}
-        ident = keep.tile([P, P], BF16, name="ident")
-        make_identity(nc, ident[:])
+        y_bank, acc = {}, {}
 
         def live(block):
             return 0 <= block < N_BLOCKS
@@ -116,25 +115,6 @@ def tile_offm_pa_t_kernel(tc, x, w1, b1, w2, b2, out):
 
         def regroup_w(copy, grouped, raw, g, q0, q1):
             regroup_weight(copy, grouped[:, g], raw[g][:], q0, q1)
-
-        def interleave_w2(g, half):
-            bank = o_psum.tile([P, 2, P, PACK], BF16, name="w2_bank", tag="acc")
-            w_bank[(g, half)] = bank
-            columns = w2_raw[g][:].rearrange("p t (q a) -> p a q t", a=PACK)
-            for i in range(2):
-                nc.tensor.matmul(
-                    bank[:, i].rearrange("p q t -> p (q t)"),
-                    ident[:],
-                    columns[:, 2 * half + i],
-                    start=True,
-                    stop=True,
-                )
-
-        def empty_w2(copy, g, half):
-            copy(
-                out=w2_grouped[:, g, 2 * half : 2 * half + 2].rearrange("p a q t -> p (a q t)"),
-                in_=w_bank[(g, half)][:].rearrange("p a q t -> p (a q t)"),
-            )
 
         def quantise_weight(grouped, codes, scales, g):
             nc.vector.quantize_mx(
@@ -176,7 +156,7 @@ def tile_offm_pa_t_kernel(tc, x, w1, b1, w2, b2, out):
             nc.vector.tensor_tensor(
                 out=z_tiles(block)[:, g, quad * QUAD : (quad + 1) * QUAD, :],
                 in0=y_bank[(block, g, quad)][:].rearrange("p a n -> p n a"),
-                in1=b1_bf[:, g, :].unsqueeze(1).to_broadcast([P, QUAD, PACK]),
+                in1=b1_f[:, g, :].unsqueeze(1).to_broadcast([P, QUAD, PACK]),
                 op=ADD,
             )
 
@@ -199,7 +179,7 @@ def tile_offm_pa_t_kernel(tc, x, w1, b1, w2, b2, out):
                     out=planes[block][:, a, 0:HALF],
                     in_=y_bank[(block, A, "pair", pair)][:, i, :],
                     func=IDENTITY,
-                    bias=b1_bf[:, A, a : a + 1],
+                    bias=b1_f[:, A, a : a + 1],
                     scale=1.0,
                 )
 
@@ -211,7 +191,7 @@ def tile_offm_pa_t_kernel(tc, x, w1, b1, w2, b2, out):
                     out=planes[block][:, a, quad * QUAD : (quad + 1) * QUAD],
                     in_=y_bank[(block, A, quad)][:, a, :],
                     func=IDENTITY,
-                    bias=b1_bf[:, A, a : a + 1],
+                    bias=b1_f[:, A, a : a + 1],
                     scale=1.0,
                 )
 
@@ -272,10 +252,10 @@ def tile_offm_pa_t_kernel(tc, x, w1, b1, w2, b2, out):
                 result = ostage.tile([P, BLOCK], F32, name="result")
                 if engine == "S":
                     nc.scalar.activation(
-                        out=result[:], in_=acc[(block, m)][:], func=IDENTITY, bias=b2_bf[:, m : m + 1], scale=1.0
+                        out=result[:], in_=acc[(block, m)][:], func=IDENTITY, bias=b2_f[:, m : m + 1], scale=1.0
                     )
                 else:
-                    nc.vector.tensor_scalar_add(out=result[:], in0=acc[(block, m)][:], scalar1=b2_bf[:, m : m + 1])
+                    nc.vector.tensor_scalar_add(out=result[:], in0=acc[(block, m)][:], scalar1=b2_f[:, m : m + 1])
                 nc.sync.dma_start(out=out_rows[b][:, m, part * BLOCK : (part + 1) * BLOCK], in_=result[:])
 
         def regroup_x_gp(block, first, last):
@@ -361,6 +341,7 @@ def tile_offm_pa_t_kernel(tc, x, w1, b1, w2, b2, out):
             regroup_w(S, w1_grouped, w1_raw, FMAP, H, P)
             regroup_w(V, w1_grouped, w1_raw, FMAP, 0, H)
             quantise_weight(w1_grouped, w1_codes, w1_scales, A)
+            nc.vector.tensor_copy(out=b1_f[:], in_=b1_bf[:])
             quantise_weight(w1_grouped, w1_codes, w1_scales, FMAP)
             regroup_x(S, 1, 2, 4)
             regroup_x(V, 1, 0, 2)
@@ -370,17 +351,13 @@ def tile_offm_pa_t_kernel(tc, x, w1, b1, w2, b2, out):
             hidden_quad(0, A, 2)
             drain_quad(0, A, 3)
             quantise_x(1)
-            interleave_w2(A, 0)
-            interleave_w2(A, 1)
             drain_pair(0, 0)
             drain_pair(0, 1)
-            empty_w2(S, A, 0)
             drain_quad_planes(0, 2)
-            empty_w2(S, A, 1)
-            interleave_w2(FMAP, 0)
             for quad in range(PACK):
                 hidden_quad(0, FMAP, quad)
-            empty_w2(S, FMAP, 0)
+            regroup_w(V, w2_grouped, w2_raw, A, 0, H)
+            regroup_w(S, w2_grouped, w2_raw, A, H, P)
             gpsimd_x(2)
             drain_quad(0, FMAP, 0)
             hidden_quad(1, A, 3)
@@ -392,13 +369,9 @@ def tile_offm_pa_t_kernel(tc, x, w1, b1, w2, b2, out):
             hidden_pair(1, 1)
             drain_quad(0, FMAP, 3)
             hidden_quad(1, A, 2)
-            interleave_w2(FMAP, 1)
-            interleave_w2(RELU, 0)
-            empty_w2(S, FMAP, 1)
-            interleave_w2(RELU, 1)
-            empty_w2(S, RELU, 0)
+            regroup_w(S, w2_grouped, w2_raw, FMAP, H, P)
+            regroup_w(S, w2_grouped, w2_raw, RELU, H, P)
             drain_quad(1, A, 3)
-            empty_w2(S, RELU, 1)
             drain_pair(1, 0)
             drain_pair(1, 1)
             hidden_quad(1, FMAP, 0)
@@ -409,6 +382,9 @@ def tile_offm_pa_t_kernel(tc, x, w1, b1, w2, b2, out):
             hidden_quad(1, FMAP, 3)
             regroup_planes(V, 0, 2)
             relu(0)
+            regroup_w(V, w2_grouped, w2_raw, FMAP, 0, H)
+            regroup_w(V, w2_grouped, w2_raw, RELU, 0, H)
+            nc.vector.tensor_copy(out=b2_f[:], in_=b2_bf[:])
             for g in range(Z_GROUPS):
                 quantise_z(0, g)
             for g in range(Z_GROUPS):

@@ -77,7 +77,7 @@ def tile_offm_pa_t_kernel(tc, x, w1, b1, w2, b2, out):
         w2_scales = keep.tile([P, Z_GROUPS, C_OUT], U8, align_bytes=64)
 
         x_grouped, x_codes, x_scales = {}, {}, {}
-        z, z_codes, z_scales, planes = {}, {}, {}, {}
+        z, z_codes, z_scales, planes, f_planes = {}, {}, {}, {}, {}
         y_bank, acc = {}, {}
 
         def live(block):
@@ -160,45 +160,63 @@ def tile_offm_pa_t_kernel(tc, x, w1, b1, w2, b2, out):
                 op=ADD,
             )
 
-        def hidden_pair(block, pair):
+        def hidden_a(block, a):
+            if not live(block):
+                return
+            y = y_psum.tile([P, BLOCK], F32, name="y_a", tag="y")
+            y_bank[(block, A, a)] = y
+            hidden_pass(y[:], block, A, a, slice(0, BLOCK))
+
+        def drain_a(block, a, engine="S"):
+            if not live(block):
+                return
+            if block not in planes:
+                planes[block] = zstage.tile([P, PACK, BLOCK], BF16, name="planes")
+            if engine == "S":
+                nc.scalar.activation(
+                    out=planes[block][:, a, :],
+                    in_=y_bank[(block, A, a)][:],
+                    func=IDENTITY,
+                    bias=b1_f[:, A, a : a + 1],
+                    scale=1.0,
+                )
+            else:
+                nc.vector.tensor_scalar_add(
+                    out=planes[block][:, a, :], in0=y_bank[(block, A, a)][:], scalar1=b1_f[:, A, a : a + 1]
+                )
+
+        def hidden_f_pair(block, pair):
             if not live(block):
                 return
             y = y_psum.tile([P, 2, HALF], F32, name="y_pair", tag="y")
-            y_bank[(block, A, "pair", pair)] = y
+            y_bank[(block, FMAP, "pair", pair)] = y
             for i in range(2):
-                hidden_pass(y[:, i, :], block, A, 2 * pair + i, slice(0, HALF))
+                hidden_pass(y[:, i, :], block, FMAP, 2 * pair + i, slice(HALF, BLOCK))
 
-        def drain_pair(block, pair):
+        def drain_f_pair(block, pair):
             if not live(block):
                 return
             if pair == 0:
-                planes[block] = zstage.tile([P, PACK, BLOCK], BF16, name="planes")
+                f_planes[block] = zstage.tile([P, PACK, HALF], BF16, name="f_planes")
             for i in range(2):
                 a = 2 * pair + i
                 nc.scalar.activation(
-                    out=planes[block][:, a, 0:HALF],
-                    in_=y_bank[(block, A, "pair", pair)][:, i, :],
+                    out=f_planes[block][:, a, :],
+                    in_=y_bank[(block, FMAP, "pair", pair)][:, i, :],
                     func=IDENTITY,
-                    bias=b1_f[:, A, a : a + 1],
+                    bias=b1_f[:, FMAP, a : a + 1],
                     scale=1.0,
                 )
 
-        def drain_quad_planes(block, quad):
-            if not live(block):
+        def regroup_f_planes(copy, block, first, last):
+            if not live(block) or first == last:
                 return
-            for a in range(PACK):
-                nc.scalar.activation(
-                    out=planes[block][:, a, quad * QUAD : (quad + 1) * QUAD],
-                    in_=y_bank[(block, A, quad)][:, a, :],
-                    func=IDENTITY,
-                    bias=b1_f[:, A, a : a + 1],
-                    scale=1.0,
-                )
+            regroup_pixels(copy, z_tiles(block)[:, FMAP, HALF + first : HALF + last, :], f_planes[block][:, :, first:last])
 
-        def regroup_planes(copy, block, quad):
+        def regroup_planes(copy, block, first, last):
             if not live(block):
                 return
-            cols = slice(quad * QUAD, (quad + 1) * QUAD)
+            cols = slice(first, last)
             regroup_pixels(copy, z_tiles(block)[:, A, cols, :], planes[block][:, :, cols])
 
         def relu(block):
@@ -210,13 +228,13 @@ def tile_offm_pa_t_kernel(tc, x, w1, b1, w2, b2, out):
                 scalar1=0.0,
             )
 
-        def quantise_z(block, g):
+        def quantise_z(block, g0, g1):
             if not live(block):
                 return
             nc.vector.quantize_mx(
-                out=z_codes[block][:, g, :].bitcast(FP8X4),
-                scales=z_scales[block][:, g, :],
-                in_=z[block][:, g].rearrange("p n t -> p (n t)"),
+                out=z_codes[block][:, g0:g1, :].rearrange("p g n -> p (g n)").bitcast(FP8X4),
+                scales=z_scales[block][:, g0:g1, :].rearrange("p g n -> p (g n)"),
+                in_=z[block][:, g0:g1].rearrange("p g n t -> p (g n t)"),
             )
 
         def output_pass(block, g, m):
@@ -266,6 +284,14 @@ def tile_offm_pa_t_kernel(tc, x, w1, b1, w2, b2, out):
             cols = slice(first, last)
             gp_copy(x_grouped[block][:, cols, :], x_raw[block][:, :, cols].rearrange("p t n -> p n t"))
 
+        def regroup_x_v(block, first, last):
+            if not live(block):
+                return
+            if block not in x_grouped:
+                x_grouped[block] = xg.tile([P, BLOCK, PACK], BF16, align_bytes=64, name="x_grouped")
+            cols = slice(first, last)
+            regroup_pixels(nc.vector.tensor_copy, x_grouped[block][:, cols, :], x_raw[block][:, :, cols])
+
         def regroup_x_s(block, first, last):
             if not live(block):
                 return
@@ -292,43 +318,49 @@ def tile_offm_pa_t_kernel(tc, x, w1, b1, w2, b2, out):
             load_x(block)
 
         def gpsimd_x(block):
-            for first in (64, 192, 320, 448):
-                regroup_x_gp(block, first, min(first + 128, BLOCK))
+            if live(block):
+                for first, last in ((128, 256), (256, 384), (384, 512), ):
+                    regroup_x_gp(block, first, last)
+
+        def v_x(block):
+            pass
+
+        def s_x(block):
+            regroup_x_s(block, 0, 128)
 
         def round_(i):
-            if i + 2 < N_BLOCKS:
-                gpsimd_x(i + 2)
-            regroup_planes(S, i, 0)
+            gpsimd_x(i + 2)
+            regroup_planes(S, i, 256, BLOCK)
             drain_quad(i, FMAP, 0)
             output_bank(i - 1, 0)
-            hidden_quad(i + 1, A, 3)
+            hidden_a(i + 1, 0)
             drain_quad(i, FMAP, 1)
-            hidden_pair(i + 1, 0)
+            hidden_a(i + 1, 1)
             drain_output(i - 1, [0], "S")
-            drain_pair(i + 1, 0)
+            drain_a(i + 1, 0)
             drain_quad(i, FMAP, 2)
             output_bank(i - 1, 1)
-            hidden_pair(i + 1, 1)
-            regroup_planes(S, i, 1)
+            hidden_a(i + 1, 2)
+            drain_a(i + 1, 1)
             drain_output(i - 1, [1], "S")
             drain_quad(i, FMAP, 3)
-            hidden_quad(i + 1, A, 2)
-            drain_pair(i + 1, 1)
-            drain_quad(i + 1, A, 3)
-            regroup_x_s(i + 2, 0, 64)
+            hidden_a(i + 1, 3)
+            drain_a(i + 1, 2)
+            v_x(i + 2)
             output_bank(i - 1, 2)
+            s_x(i + 2)
             hidden_quad(i + 1, FMAP, 0)
             hidden_quad(i + 1, FMAP, 1)
+            drain_a(i + 1, 3)
             drain_output(i - 1, [2], "S")
-            drain_quad_planes(i + 1, 2)
             output_bank(i - 1, 3)
             hidden_quad(i + 1, FMAP, 2)
             hidden_quad(i + 1, FMAP, 3)
             drain_output(i - 1, [3], "S")
-            regroup_planes(V, i, 2)
+            regroup_planes(V, i, 0, 256)
             relu(i)
-            for g in range(Z_GROUPS):
-                quantise_z(i, g)
+            quantise_z(i, A, RELU)
+            quantise_z(i, RELU, RELU + 1)
             quantise_x(i + 2)
 
         with tc.manual_schedule():
@@ -343,65 +375,66 @@ def tile_offm_pa_t_kernel(tc, x, w1, b1, w2, b2, out):
             quantise_weight(w1_grouped, w1_codes, w1_scales, A)
             nc.vector.tensor_copy(out=b1_f[:], in_=b1_bf[:])
             quantise_weight(w1_grouped, w1_codes, w1_scales, FMAP)
-            regroup_x(S, 1, 2, 4)
-            regroup_x(V, 1, 0, 2)
-            hidden_quad(0, A, 3)
-            hidden_pair(0, 0)
-            hidden_pair(0, 1)
-            hidden_quad(0, A, 2)
-            drain_quad(0, A, 3)
+            for a in range(PACK):
+                hidden_a(0, a)
+            regroup_x(S, 1, 3, 4)
+            regroup_x(V, 1, 0, 3)
+            drain_a(0, 0)
+            hidden_quad(0, FMAP, 0)
+            drain_a(0, 1)
+            hidden_quad(0, FMAP, 1)
             quantise_x(1)
-            drain_pair(0, 0)
-            drain_pair(0, 1)
-            drain_quad_planes(0, 2)
-            for quad in range(PACK):
-                hidden_quad(0, FMAP, quad)
-            regroup_w(V, w2_grouped, w2_raw, A, 0, H)
-            regroup_w(S, w2_grouped, w2_raw, A, H, P)
-            gpsimd_x(2)
             drain_quad(0, FMAP, 0)
-            hidden_quad(1, A, 3)
-            regroup_planes(S, 0, 0)
+            drain_a(0, 2)
+            hidden_quad(0, FMAP, 2)
             drain_quad(0, FMAP, 1)
-            hidden_pair(1, 0)
-            regroup_planes(S, 0, 1)
+            drain_a(0, 3)
+            hidden_quad(0, FMAP, 3)
+            gpsimd_x(2)
+            hidden_a(1, 0)
+            hidden_a(1, 1)
             drain_quad(0, FMAP, 2)
-            hidden_pair(1, 1)
+            regroup_w(S, w2_grouped, w2_raw, A, H, P)
+            regroup_w(V, w2_grouped, w2_raw, A, 0, H)
+            hidden_a(1, 2)
             drain_quad(0, FMAP, 3)
-            hidden_quad(1, A, 2)
-            regroup_w(S, w2_grouped, w2_raw, FMAP, H, P)
-            regroup_w(S, w2_grouped, w2_raw, RELU, H, P)
-            drain_quad(1, A, 3)
-            drain_pair(1, 0)
-            drain_pair(1, 1)
+            hidden_a(1, 3)
+            regroup_planes(S, 0, 256, BLOCK)
+            regroup_planes(V, 0, 0, 256)
+            drain_a(1, 0)
+            drain_a(1, 1)
             hidden_quad(1, FMAP, 0)
             hidden_quad(1, FMAP, 1)
-            hidden_quad(1, FMAP, 2)
-            regroup_x_s(2, 0, 64)
-            drain_quad_planes(1, 2)
-            hidden_quad(1, FMAP, 3)
-            regroup_planes(V, 0, 2)
             relu(0)
+            regroup_w(S, w2_grouped, w2_raw, FMAP, H, P)
+            regroup_w(S, w2_grouped, w2_raw, RELU, H, P)
+            drain_a(1, 2)
+            drain_a(1, 3)
+            hidden_quad(1, FMAP, 2)
+            hidden_quad(1, FMAP, 3)
+
+            s_x(2)
+            v_x(2)
             regroup_w(V, w2_grouped, w2_raw, FMAP, 0, H)
             regroup_w(V, w2_grouped, w2_raw, RELU, 0, H)
             nc.vector.tensor_copy(out=b2_f[:], in_=b2_bf[:])
-            for g in range(Z_GROUPS):
-                quantise_z(0, g)
+            quantise_z(0, A, RELU)
+            quantise_z(0, RELU, RELU + 1)
             for g in range(Z_GROUPS):
                 quantise_weight(w2_grouped, w2_codes, w2_scales, g)
             quantise_x(2)
             for i in range(1, N_BLOCKS - 1):
                 round_(i)
             i = N_BLOCKS - 1
-            regroup_planes(S, i, 0)
-            regroup_planes(S, i, 1)
-            regroup_planes(V, i, 2)
+            regroup_planes(S, i, 256, BLOCK)
+            regroup_planes(V, i, 0, 256)
+
             output_bank(i - 1, 0)
             drain_quad(i, FMAP, 0)
             drain_output(i - 1, [0], "S")
             drain_quad(i, FMAP, 1)
             output_bank(i - 1, 1)
-            quantise_z(i, A)
+            quantise_z(i, A, FMAP)
             drain_output(i - 1, [1], "S")
             drain_quad(i, FMAP, 2)
             output_bank(i - 1, 2)
@@ -411,9 +444,9 @@ def tile_offm_pa_t_kernel(tc, x, w1, b1, w2, b2, out):
             relu(i)
             drain_output(i - 1, [3], "S")
             output_group_last(A)
-            quantise_z(i, FMAP)
+            quantise_z(i, FMAP, RELU)
             output_group_last(FMAP)
-            quantise_z(i, RELU)
+            quantise_z(i, RELU, RELU + 1)
             output_group_last(RELU)
             for m in range(PACK):
                 drain_output(i, [m], "VS"[m % 2])

@@ -15,19 +15,31 @@ P = 128
 PACK = 4
 K_PASS = P * PACK
 
-IMAGES = 4
 C_IN = 512
 HIDDEN = 1024
 PIXELS = 1024
+IMAGES = 4
 C_OUT = 512
 Y_GROUPS = HIDDEN // K_PASS
 Z_GROUPS = Y_GROUPS + 1
 A, FMAP, RELU = 0, 1, 2
-BLOCK = 512
-QUAD = BLOCK // PACK
-HALF = BLOCK // 2
-BLOCKS_PER_IMAGE = PIXELS // BLOCK
-N_BLOCKS = IMAGES * BLOCKS_PER_IMAGE
+WIDE = 512
+HALF = WIDE // 2
+QUAD = WIDE // PACK
+
+BLOCKS = [
+    (0, 0, 256, 1),
+    (0, 256, 256, 1),
+    (0, 512, 512, 1),
+    (1, 0, 512, 1),
+    (1, 512, 512, 1),
+    (2, 0, 512, 1),
+    (2, 512, 512, 1),
+    (3, 0, 512, 1),
+    (3, 512, 256, 1),
+    (3, 768, 256, 1),
+]
+N_BLOCKS = len(BLOCKS)
 
 FLOPS = 2 * IMAGES * PIXELS * (C_IN * HIDDEN + Z_GROUPS * K_PASS * C_OUT)
 
@@ -39,10 +51,10 @@ def regroup_pixels(copy, grouped, rows):
     )
 
 
-def regroup_weight(copy, grouped, rows, q0=0, q1=P):
+def regroup_weight(copy, grouped, rows, first, last):
     copy(
-        out=grouped[:, :, q0:q1, :].rearrange("p a q t -> p q t a"),
-        in_=rows[:, :, PACK * q0 : PACK * q1].rearrange("p t (q a) -> p q t a", a=PACK),
+        out=grouped[:, first:last].rearrange("p a q t -> p q t a"),
+        in_=rows.rearrange("p t (q a) -> p q t a", a=PACK)[:, :, :, first:last],
     )
 
 
@@ -68,7 +80,7 @@ def tile_offm_pa_t_kernel(tc, x, w1, b1, w2, b2, out):
         b2_f = keep.tile([P, PACK], F32)
         w1_raw = [keep.tile([P, PACK, K_PASS], BF16, name="w1_raw%d" % g) for g in range(Y_GROUPS)]
         w2_raw = [keep.tile([P, PACK, C_OUT], BF16, name="w2_raw%d" % g) for g in range(Z_GROUPS)]
-        x_raw = [keep.tile([P, PACK, BLOCK], BF16, name="x_raw%d" % i) for i in range(N_BLOCKS)]
+        x_raw = [keep.tile([P, PACK, BLOCKS[i][2]], BF16, name="x_raw%d" % i) for i in range(N_BLOCKS)]
         w1_grouped = keep.tile([P, Y_GROUPS, PACK, P, PACK], BF16, align_bytes=64)
         w2_grouped = keep.tile([P, Z_GROUPS, PACK, P, PACK], BF16, align_bytes=64)
         w1_codes = keep.tile([P, Y_GROUPS, K_PASS], U32, align_bytes=64)
@@ -77,16 +89,24 @@ def tile_offm_pa_t_kernel(tc, x, w1, b1, w2, b2, out):
         w2_scales = keep.tile([P, Z_GROUPS, C_OUT], U8, align_bytes=64)
 
         x_grouped, x_codes, x_scales = {}, {}, {}
-        z, z_codes, z_scales, planes, f_planes = {}, {}, {}, {}, {}
+        z, z_codes, z_scales, planes, f_pairs = {}, {}, {}, {}, {}
         y_bank, acc = {}, {}
+        drained = set([])
+
+        V, S = nc.vector.tensor_copy, nc.scalar.copy
+
+        def G(out, in_):
+            nc.gpsimd.tensor_scalar(out=out, in0=in_, scalar1=1.0, scalar2=0.0, op0=MULT, op1=ADD)
 
         def live(block):
             return 0 <= block < N_BLOCKS
 
+        def width(block):
+            return BLOCKS[block][2]
+
         def load_x(block):
-            b, part = divmod(block, BLOCKS_PER_IMAGE)
-            cols = slice(part * BLOCK, (part + 1) * BLOCK)
-            nc.sync.dma_start(out=x_raw[block][:], in_=x_rows[b][:, :, cols])
+            b, first, w = BLOCKS[block][:3]
+            nc.sync.dma_start(out=x_raw[block][:], in_=x_rows[b][:, :, first : first + w])
 
         def load_w1(g):
             nc.sync.dma_start(out=w1_raw[g][:], in_=w1_rows[:, :, g * K_PASS : (g + 1) * K_PASS])
@@ -95,26 +115,33 @@ def tile_offm_pa_t_kernel(tc, x, w1, b1, w2, b2, out):
             nc.sync.dma_start(out=w2_raw[g][:], in_=w2_rows[g])
 
         def regroup_x(copy, block, first, last):
-            if not live(block):
+            if not live(block) or first >= last:
                 return
             if block not in x_grouped:
-                x_grouped[block] = xg.tile([P, BLOCK, PACK], BF16, align_bytes=64, name="x_grouped")
-            cols = slice(first * QUAD, last * QUAD)
-            regroup_pixels(copy, x_grouped[block][:, cols, :], x_raw[block][:, :, cols])
+                x_grouped[block] = xg.tile([P, width(block), PACK], BF16, align_bytes=64, name="x_grouped")
+            cols = slice(first, last)
+            if copy is G:
+                G(out=x_grouped[block][:, cols, :], in_=x_raw[block][:, :, cols].rearrange("p t n -> p n t"))
+            else:
+                regroup_pixels(copy, x_grouped[block][:, cols, :], x_raw[block][:, :, cols])
 
         def quantise_x(block):
             if not live(block):
                 return
-            x_codes[block] = xstage.tile([P, BLOCK], U32, align_bytes=64, name="x_codes")
-            x_scales[block] = xstage.tile([P, BLOCK], U8, align_bytes=64, name="x_scales")
+            x_codes[block] = xstage.tile([P, width(block)], U32, align_bytes=64, name="x_codes")
+            x_scales[block] = xstage.tile([P, width(block)], U8, align_bytes=64, name="x_scales")
             nc.vector.quantize_mx(
                 out=x_codes[block][:].bitcast(FP8X4),
                 scales=x_scales[block][:],
                 in_=x_grouped[block][:].rearrange("p n t -> p (n t)"),
             )
 
-        def regroup_w(copy, grouped, raw, g, q0, q1):
-            regroup_weight(copy, grouped[:, g], raw[g][:], q0, q1)
+        def regroup_w1(copy, g, first, last):
+            regroup_weight(copy, w1_grouped[:, g], w1_raw[g][:], first, last)
+
+        def regroup_w2(copy, g, first, last):
+            if first < last:
+                regroup_weight(copy, w2_grouped[:, g], w2_raw[g][:], first, last)
 
         def quantise_weight(grouped, codes, scales, g):
             nc.vector.quantize_mx(
@@ -122,6 +149,12 @@ def tile_offm_pa_t_kernel(tc, x, w1, b1, w2, b2, out):
                 scales=scales[:, g, :],
                 in_=grouped[:, g].rearrange("p a q t -> p (a q t)"),
             )
+
+        def quantise_w1(g):
+            quantise_weight(w1_grouped, w1_codes, w1_scales, g)
+
+        def quantise_w2(g):
+            quantise_weight(w2_grouped, w2_codes, w2_scales, g)
 
         def hidden_pass(y_part, block, g, a, cols):
             w_cols = slice(a * P, (a + 1) * P)
@@ -135,98 +168,117 @@ def tile_offm_pa_t_kernel(tc, x, w1, b1, w2, b2, out):
                 stop=True,
             )
 
-        def hidden_quad(block, g, quad):
-            if not live(block):
-                return
-            y = y_psum.tile([P, PACK, QUAD], F32, name="y_quad", tag="y")
-            y_bank[(block, g, quad)] = y
-            for a in range(PACK):
-                hidden_pass(y[:, a, :], block, g, a, slice(quad * QUAD, (quad + 1) * QUAD))
-
         def z_tiles(block):
             if block not in z:
-                z[block] = zstage.tile([P, Z_GROUPS, BLOCK, PACK], BF16, align_bytes=64, name="z")
-                z_codes[block] = zstage.tile([P, Z_GROUPS, BLOCK], U32, align_bytes=64, name="z_codes")
-                z_scales[block] = zstage.tile([P, Z_GROUPS, BLOCK], U8, align_bytes=64, name="z_scales")
+                w = width(block)
+                z[block] = zstage.tile([P, Z_GROUPS, w, PACK], BF16, align_bytes=64, name="z")
+                z_codes[block] = zstage.tile([P, Z_GROUPS, w], U32, align_bytes=64, name="z_codes")
+                z_scales[block] = zstage.tile([P, Z_GROUPS, w], U8, align_bytes=64, name="z_scales")
             return z[block]
 
-        def drain_quad(block, g, quad):
-            if not live(block):
+        def direct(block, h):
+            return h < BLOCKS[block][3]
+
+        def hidden_f(block, h, j):
+            if not live(block) or h * HALF >= width(block):
                 return
+            if direct(block, h):
+                y = y_psum.tile([P, PACK, QUAD], F32, name="y_quad", tag="y")
+                y_bank[(block, "f", h, j)] = y
+                first = h * HALF + j * QUAD
+                for a in range(PACK):
+                    hidden_pass(y[:, a, :], block, FMAP, a, slice(first, first + QUAD))
+                return
+            y = y_psum.tile([P, 2, HALF], F32, name="y_f", tag="y")
+            y_bank[(block, "f", h, j)] = y
+            for i in range(2):
+                hidden_pass(y[:, i, :], block, FMAP, 2 * j + i, slice(h * HALF, (h + 1) * HALF))
+
+        def drain_f(block, h, j):
+            if not live(block) or h * HALF >= width(block):
+                return
+            if direct(block, h):
+                first = h * HALF + j * QUAD
+                nc.vector.tensor_tensor(
+                    out=z_tiles(block)[:, FMAP, first : first + QUAD, :],
+                    in0=y_bank[(block, "f", h, j)][:].rearrange("p a n -> p n a"),
+                    in1=b1_f[:, FMAP, :].unsqueeze(1).to_broadcast([P, QUAD, PACK]),
+                    op=ADD,
+                )
+                return
+            if block not in f_pairs:
+                f_pairs[block] = zstage.tile([P, 2, width(block), 2], BF16, align_bytes=64, name="f_pairs")
             nc.vector.tensor_tensor(
-                out=z_tiles(block)[:, g, quad * QUAD : (quad + 1) * QUAD, :],
-                in0=y_bank[(block, g, quad)][:].rearrange("p a n -> p n a"),
-                in1=b1_f[:, g, :].unsqueeze(1).to_broadcast([P, QUAD, PACK]),
+                out=f_pairs[block][:, j, h * HALF : (h + 1) * HALF, :],
+                in0=y_bank[(block, "f", h, j)][:].rearrange("p a n -> p n a"),
+                in1=b1_f[:, FMAP, 2 * j : 2 * j + 2].unsqueeze(1).to_broadcast([P, HALF, 2]),
                 op=ADD,
             )
 
-        def hidden_a(block, a):
-            if not live(block):
+        def join_f(copy, block, h):
+            if not live(block) or h * HALF >= width(block) or direct(block, h):
                 return
-            y = y_psum.tile([P, BLOCK], F32, name="y_a", tag="y")
-            y_bank[(block, A, a)] = y
-            hidden_pass(y[:], block, A, a, slice(0, BLOCK))
+            cols = slice(h * HALF, (h + 1) * HALF)
+            copy(
+                out=z_tiles(block)[:, FMAP, cols, :].rearrange("p n (j i) -> p n j i", i=2),
+                in_=f_pairs[block][:, :, cols, :].rearrange("p j n i -> p n j i"),
+            )
 
-        def drain_a(block, a, engine="S"):
-            if not live(block):
+        def hidden_planes(block, g, a):
+            if not live(block) or (block, g, a) in y_bank:
                 return
-            if block not in planes:
-                planes[block] = zstage.tile([P, PACK, BLOCK], BF16, name="planes")
-            if engine == "S":
-                nc.scalar.activation(
-                    out=planes[block][:, a, :],
-                    in_=y_bank[(block, A, a)][:],
-                    func=IDENTITY,
-                    bias=b1_f[:, A, a : a + 1],
-                    scale=1.0,
-                )
-            else:
-                nc.vector.tensor_scalar_add(
-                    out=planes[block][:, a, :], in0=y_bank[(block, A, a)][:], scalar1=b1_f[:, A, a : a + 1]
-                )
+            w = width(block)
+            per_bank = WIDE // w
+            if a % per_bank:
+                return
+            y = y_psum.tile([P, per_bank, w], F32, name="y_planes", tag="y")
+            for i in range(per_bank):
+                y_bank[(block, g, a + i)] = y[:, i, :]
+                hidden_pass(y[:, i, :], block, g, a + i, slice(0, w))
 
-        def hidden_f_pair(block, pair):
-            if not live(block):
+        def drain_planes(block, g, a, engine="S"):
+            if not live(block) or (block, g, a) in drained:
                 return
-            y = y_psum.tile([P, 2, HALF], F32, name="y_pair", tag="y")
-            y_bank[(block, FMAP, "pair", pair)] = y
-            for i in range(2):
-                hidden_pass(y[:, i, :], block, FMAP, 2 * pair + i, slice(HALF, BLOCK))
+            drained.add((block, g, a))
+            store = planes
+            w = width(block)
+            if block not in store:
+                store[block] = zstage.tile([P, PACK, w], BF16, name="planes")
+            per_bank = WIDE // w
+            if a % per_bank:
+                return
+            for i in range(a, a + per_bank):
+                if engine == "S":
+                    nc.scalar.activation(
+                        out=store[block][:, i, :], in_=y_bank[(block, g, i)], func=IDENTITY,
+                        bias=b1_f[:, g, i : i + 1], scale=1.0,
+                    )
+                else:
+                    nc.vector.tensor_scalar_add(
+                        out=store[block][:, i, :], in0=y_bank[(block, g, i)], scalar1=b1_f[:, g, i : i + 1]
+                    )
 
-        def drain_f_pair(block, pair):
-            if not live(block):
+        def regroup_planes(copy, block, g, first, last):
+            if not live(block) or first >= last:
                 return
-            if pair == 0:
-                f_planes[block] = zstage.tile([P, PACK, HALF], BF16, name="f_planes")
-            for i in range(2):
-                a = 2 * pair + i
-                nc.scalar.activation(
-                    out=f_planes[block][:, a, :],
-                    in_=y_bank[(block, FMAP, "pair", pair)][:, i, :],
-                    func=IDENTITY,
-                    bias=b1_f[:, FMAP, a : a + 1],
-                    scale=1.0,
-                )
-
-        def regroup_f_planes(copy, block, first, last):
-            if not live(block) or first == last:
-                return
-            regroup_pixels(copy, z_tiles(block)[:, FMAP, HALF + first : HALF + last, :], f_planes[block][:, :, first:last])
-
-        def regroup_planes(copy, block, first, last):
-            if not live(block):
-                return
-            cols = slice(first, last)
-            regroup_pixels(copy, z_tiles(block)[:, A, cols, :], planes[block][:, :, cols])
+            regroup_pixels(copy, z_tiles(block)[:, g, first:last, :], planes[block][:, :, first:last])
 
         def relu(block):
             if not live(block):
                 return
-            nc.vector.tensor_scalar_max(
-                out=z[block][:, RELU].rearrange("p n t -> p (n t)"),
-                in0=z[block][:, FMAP].rearrange("p n t -> p (n t)"),
-                scalar1=0.0,
-            )
+            split = BLOCKS[block][3] * HALF
+            if split > 0:
+                nc.vector.tensor_scalar_max(
+                    out=z_tiles(block)[:, RELU, 0:split].rearrange("p n t -> p (n t)"),
+                    in0=z_tiles(block)[:, FMAP, 0:split].rearrange("p n t -> p (n t)"),
+                    scalar1=0.0,
+                )
+            if split < width(block):
+                nc.vector.tensor_scalar_max(
+                    out=z_tiles(block)[:, RELU, split:].rearrange("p n (j i) -> p n j i", i=2),
+                    in0=f_pairs[block][:, :, split:, :].rearrange("p j n i -> p n j i"),
+                    scalar1=0.0,
+                )
 
         def quantise_z(block, g0, g1):
             if not live(block):
@@ -252,201 +304,178 @@ def tile_offm_pa_t_kernel(tc, x, w1, b1, w2, b2, out):
         def output_bank(block, m):
             if not live(block):
                 return
-            acc[(block, m)] = o_psum.tile([P, BLOCK], F32, name="acc")
+            acc[(block, m)] = o_psum.tile([P, width(block)], F32, name="acc")
             for g in range(Z_GROUPS):
                 output_pass(block, g, m)
 
         def output_group_last(g):
+            block = N_BLOCKS - 1
             for m in range(PACK):
                 if g == 0:
-                    acc[(N_BLOCKS - 1, m)] = y_psum.tile([P, BLOCK], F32, name="acc_last", tag="y")
-                output_pass(N_BLOCKS - 1, g, m)
+                    acc[(block, m)] = y_psum.tile([P, width(block)], F32, name="acc_last", tag="y")
+                output_pass(block, g, m)
 
-        def drain_output(block, banks, engine):
+        def drain_output(block, m, engine):
             if not live(block):
                 return
-            b, part = divmod(block, BLOCKS_PER_IMAGE)
-            for m in banks:
-                result = ostage.tile([P, BLOCK], F32, name="result")
-                if engine == "S":
-                    nc.scalar.activation(
-                        out=result[:], in_=acc[(block, m)][:], func=IDENTITY, bias=b2_f[:, m : m + 1], scale=1.0
-                    )
-                else:
-                    nc.vector.tensor_scalar_add(out=result[:], in0=acc[(block, m)][:], scalar1=b2_f[:, m : m + 1])
-                nc.sync.dma_start(out=out_rows[b][:, m, part * BLOCK : (part + 1) * BLOCK], in_=result[:])
+            b, first, w = BLOCKS[block][:3]
+            result = ostage.tile([P, w], F32, name="result")
+            if engine == "S":
+                nc.scalar.activation(
+                    out=result[:], in_=acc[(block, m)][:], func=IDENTITY, bias=b2_f[:, m : m + 1], scale=1.0
+                )
+            else:
+                nc.vector.tensor_scalar_add(out=result[:], in0=acc[(block, m)][:], scalar1=b2_f[:, m : m + 1])
+            nc.sync.dma_start(out=out_rows[b][:, m, first : first + w], in_=result[:])
 
-        def regroup_x_gp(block, first, last):
-            if not live(block):
-                return
-            if block not in x_grouped:
-                x_grouped[block] = xg.tile([P, BLOCK, PACK], BF16, align_bytes=64, name="x_grouped")
-            cols = slice(first, last)
-            gp_copy(x_grouped[block][:, cols, :], x_raw[block][:, :, cols].rearrange("p t n -> p n t"))
-
-        def regroup_x_v(block, first, last):
-            if not live(block):
-                return
-            if block not in x_grouped:
-                x_grouped[block] = xg.tile([P, BLOCK, PACK], BF16, align_bytes=64, name="x_grouped")
-            cols = slice(first, last)
-            regroup_pixels(nc.vector.tensor_copy, x_grouped[block][:, cols, :], x_raw[block][:, :, cols])
-
-        def regroup_x_s(block, first, last):
-            if not live(block):
-                return
-            if block not in x_grouped:
-                x_grouped[block] = xg.tile([P, BLOCK, PACK], BF16, align_bytes=64, name="x_grouped")
-            cols = slice(first, last)
-            regroup_pixels(nc.scalar.copy, x_grouped[block][:, cols, :], x_raw[block][:, :, cols])
-
-        def gp_copy(out, in_):
-            nc.gpsimd.tensor_scalar(out=out, in0=in_, scalar1=1.0, scalar2=0.0, op0=MULT, op1=ADD)
-
-        V, S = nc.vector.tensor_copy, nc.scalar.copy
-
-        load_x(0)
         load_w1(A)
+        load_x(0)
         load_w1(FMAP)
         nc.sync.dma_start(out=b1_bf[:], in_=b1.rearrange("(g p a) -> p g a", g=Y_GROUPS, a=PACK))
         load_x(1)
         load_w2(A)
+        load_x(2)
         load_w2(FMAP)
         load_w2(RELU)
         nc.sync.dma_start(out=b2_bf[:], in_=b2.rearrange("(p m) -> p m", m=PACK))
-        for block in range(2, N_BLOCKS):
+        for block in range(3, N_BLOCKS):
             load_x(block)
+
+        V_A = {WIDE: 192, HALF: 128}
+        X_S = {WIDE: 128, HALF: 64}
+        X_V = {WIDE: 128, HALF: 64}
 
         def gpsimd_x(block):
             if live(block):
-                for first, last in ((128, 256), (256, 384), (384, 512), ):
-                    regroup_x_gp(block, first, last)
+                w = width(block)
+                for first in range(X_V[w], w, 128):
+                    regroup_x(G, block, first, min(first + 128, w))
 
-        def v_x(block):
-            pass
+        def scalar_x(block):
+            if live(block):
+                regroup_x(S, block, 0, X_S[width(block)])
 
-        def s_x(block):
-            regroup_x_s(block, 0, 128)
+        def vector_x(block):
+            if live(block):
+                regroup_x(V, block, X_S[width(block)], X_V[width(block)])
+
+        def scalar_planes(i):
+            if live(i):
+                regroup_planes(S, i, A, V_A[width(i)], width(i))
+
+        def vector_planes(i):
+            if live(i):
+                regroup_planes(V, i, A, 0, V_A[width(i)])
+
+        def join(i):
+            join_f(V, i, 0)
+            join_f(V, i, 1)
 
         def round_(i):
             gpsimd_x(i + 2)
-            regroup_planes(S, i, 256, BLOCK)
-            drain_quad(i, FMAP, 0)
+            scalar_planes(i)
+            drain_f(i, 0, 0)
             output_bank(i - 1, 0)
-            hidden_a(i + 1, 0)
-            drain_quad(i, FMAP, 1)
-            hidden_a(i + 1, 1)
-            drain_output(i - 1, [0], "S")
-            drain_a(i + 1, 0)
-            drain_quad(i, FMAP, 2)
+            hidden_planes(i + 1, A, 0)
+            drain_f(i, 0, 1)
+            hidden_planes(i + 1, A, 1)
+            drain_output(i - 1, 0, "S")
+            drain_planes(i + 1, A, 0)
+            drain_f(i, 1, 0)
             output_bank(i - 1, 1)
-            hidden_a(i + 1, 2)
-            drain_a(i + 1, 1)
-            drain_output(i - 1, [1], "S")
-            drain_quad(i, FMAP, 3)
-            hidden_a(i + 1, 3)
-            drain_a(i + 1, 2)
-            v_x(i + 2)
+            hidden_planes(i + 1, A, 2)
+            drain_planes(i + 1, A, 1)
+            drain_output(i - 1, 1, "S")
+            drain_f(i, 1, 1)
+            hidden_planes(i + 1, A, 3)
+            drain_planes(i + 1, A, 2)
+            vector_planes(i)
+            vector_x(i + 2)
             output_bank(i - 1, 2)
-            s_x(i + 2)
-            hidden_quad(i + 1, FMAP, 0)
-            hidden_quad(i + 1, FMAP, 1)
-            drain_a(i + 1, 3)
-            drain_output(i - 1, [2], "S")
+            scalar_x(i + 2)
+            hidden_f(i + 1, 0, 0)
+            drain_planes(i + 1, A, 3)
+            hidden_f(i + 1, 0, 1)
+            drain_output(i - 1, 2, "S")
             output_bank(i - 1, 3)
-            hidden_quad(i + 1, FMAP, 2)
-            hidden_quad(i + 1, FMAP, 3)
-            drain_output(i - 1, [3], "S")
-            regroup_planes(V, i, 0, 256)
+            hidden_f(i + 1, 1, 0)
+            hidden_f(i + 1, 1, 1)
+            drain_output(i - 1, 3, "S")
             relu(i)
-            quantise_z(i, A, RELU)
+            join(i)
             quantise_z(i, RELU, RELU + 1)
+            quantise_z(i, A, RELU)
             quantise_x(i + 2)
 
         with tc.manual_schedule():
-            H = 80
-            regroup_x(V, 0, 0, 3)
-            regroup_x(S, 0, 3, 4)
+            regroup_w1(V, A, 0, 2)
+            regroup_w1(S, A, 2, PACK)
+            regroup_x(V, 0, 0, HALF)
+            quantise_w1(A)
             quantise_x(0)
-            regroup_w(S, w1_grouped, w1_raw, A, H, P)
-            regroup_w(V, w1_grouped, w1_raw, A, 0, H)
-            regroup_w(S, w1_grouped, w1_raw, FMAP, H, P)
-            regroup_w(V, w1_grouped, w1_raw, FMAP, 0, H)
-            quantise_weight(w1_grouped, w1_codes, w1_scales, A)
+            hidden_planes(0, A, 0)
+            hidden_planes(0, A, 2)
+            regroup_w1(V, FMAP, 0, 2)
+            regroup_w1(S, FMAP, 2, PACK)
             nc.vector.tensor_copy(out=b1_f[:], in_=b1_bf[:])
-            quantise_weight(w1_grouped, w1_codes, w1_scales, FMAP)
-            for a in range(PACK):
-                hidden_a(0, a)
-            regroup_x(S, 1, 3, 4)
-            regroup_x(V, 1, 0, 3)
-            drain_a(0, 0)
-            hidden_quad(0, FMAP, 0)
-            drain_a(0, 1)
-            hidden_quad(0, FMAP, 1)
+            regroup_x(V, 1, 0, HALF)
+            quantise_w1(FMAP)
             quantise_x(1)
-            drain_quad(0, FMAP, 0)
-            drain_a(0, 2)
-            hidden_quad(0, FMAP, 2)
-            drain_quad(0, FMAP, 1)
-            drain_a(0, 3)
-            hidden_quad(0, FMAP, 3)
-            gpsimd_x(2)
-            hidden_a(1, 0)
-            hidden_a(1, 1)
-            drain_quad(0, FMAP, 2)
-            regroup_w(S, w2_grouped, w2_raw, A, H, P)
-            regroup_w(V, w2_grouped, w2_raw, A, 0, H)
-            hidden_a(1, 2)
-            drain_quad(0, FMAP, 3)
-            hidden_a(1, 3)
-            regroup_planes(S, 0, 256, BLOCK)
-            regroup_planes(V, 0, 0, 256)
-            drain_a(1, 0)
-            drain_a(1, 1)
-            hidden_quad(1, FMAP, 0)
-            hidden_quad(1, FMAP, 1)
+            hidden_f(0, 0, 0)
+            hidden_f(0, 0, 1)
+            drain_planes(0, A, 0)
+            drain_planes(0, A, 2)
+            regroup_w2(V, A, 0, 1)
+            regroup_w2(S, A, 1, PACK)
+            drain_f(0, 0, 0)
+            hidden_planes(1, A, 0)
+            hidden_planes(1, A, 2)
+            drain_f(0, 0, 1)
+            regroup_planes(V, 0, A, 0, HALF)
+            hidden_f(1, 0, 0)
+            hidden_f(1, 0, 1)
             relu(0)
-            regroup_w(S, w2_grouped, w2_raw, FMAP, H, P)
-            regroup_w(S, w2_grouped, w2_raw, RELU, H, P)
-            drain_a(1, 2)
-            drain_a(1, 3)
-            hidden_quad(1, FMAP, 2)
-            hidden_quad(1, FMAP, 3)
-
-            s_x(2)
-            v_x(2)
-            regroup_w(V, w2_grouped, w2_raw, FMAP, 0, H)
-            regroup_w(V, w2_grouped, w2_raw, RELU, 0, H)
-            nc.vector.tensor_copy(out=b2_f[:], in_=b2_bf[:])
-            quantise_z(0, A, RELU)
-            quantise_z(0, RELU, RELU + 1)
-            for g in range(Z_GROUPS):
-                quantise_weight(w2_grouped, w2_codes, w2_scales, g)
+            join_f(V, 0, 0)
+            quantise_w2(A)
+            regroup_x(S, 2, 256, WIDE)
+            regroup_x(V, 2, 0, 256)
+            drain_planes(1, A, 0)
+            regroup_w2(V, FMAP, 0, 2)
+            regroup_w2(S, FMAP, 2, PACK)
             quantise_x(2)
+            quantise_z(0, RELU, RELU + 1)
+            quantise_z(0, A, RELU)
+            hidden_planes(2, A, 0)
+            hidden_planes(2, A, 1)
+            regroup_w2(V, RELU, 0, 2)
+            regroup_w2(S, RELU, 2, PACK)
+            drain_planes(1, A, 2)
+            quantise_w2(FMAP)
+            nc.vector.tensor_copy(out=b2_f[:], in_=b2_bf[:])
+            drain_planes(2, A, 0)
+            quantise_w2(RELU)
             for i in range(1, N_BLOCKS - 1):
                 round_(i)
             i = N_BLOCKS - 1
-            regroup_planes(S, i, 256, BLOCK)
-            regroup_planes(V, i, 0, 256)
-
+            scalar_planes(i)
+            vector_planes(i)
             output_bank(i - 1, 0)
-            drain_quad(i, FMAP, 0)
-            drain_output(i - 1, [0], "S")
-            drain_quad(i, FMAP, 1)
+            drain_f(i, 0, 0)
+            drain_output(i - 1, 0, "S")
+            drain_f(i, 0, 1)
             output_bank(i - 1, 1)
             quantise_z(i, A, FMAP)
-            drain_output(i - 1, [1], "S")
-            drain_quad(i, FMAP, 2)
+            drain_output(i - 1, 1, "S")
             output_bank(i - 1, 2)
-            drain_quad(i, FMAP, 3)
-            drain_output(i - 1, [2], "S")
-            output_bank(i - 1, 3)
+            drain_output(i - 1, 2, "S")
+            join_f(V, i, 0)
             relu(i)
-            drain_output(i - 1, [3], "S")
+            output_bank(i - 1, 3)
+            drain_output(i - 1, 3, "S")
             output_group_last(A)
             quantise_z(i, FMAP, RELU)
             output_group_last(FMAP)
             quantise_z(i, RELU, RELU + 1)
             output_group_last(RELU)
             for m in range(PACK):
-                drain_output(i, [m], "VS"[m % 2])
+                drain_output(i, m, "VS"[m % 2])

@@ -30,12 +30,12 @@ QUAD = WIDE // PACK
 BLOCKS = [
     (0, 0, 256, 1),
     (0, 256, 256, 1),
-    (0, 512, 512, 1),
-    (1, 0, 512, 1),
-    (1, 512, 512, 1),
-    (2, 0, 512, 1),
-    (2, 512, 512, 1),
-    (3, 0, 512, 1),
+    (0, 512, 512, 2),
+    (1, 0, 512, 2),
+    (1, 512, 512, 2),
+    (2, 0, 512, 2),
+    (2, 512, 512, 2),
+    (3, 0, 512, 2),
     (3, 512, 256, 1),
     (3, 768, 256, 1),
 ]

@@ -28,16 +28,16 @@ HALF = WIDE // 2
 QUAD = WIDE // PACK
 
 BLOCKS = [
-    (0, 0, 256, 1),
-    (0, 256, 256, 1),
-    (0, 512, 512, 2),
-    (1, 0, 512, 2),
-    (1, 512, 512, 2),
-    (2, 0, 512, 2),
-    (2, 512, 512, 2),
-    (3, 0, 512, 2),
-    (3, 512, 256, 1),
-    (3, 768, 256, 1),
+    (0, 0, 256),
+    (0, 256, 256),
+    (0, 512, 512),
+    (1, 0, 512),
+    (1, 512, 512),
+    (2, 0, 512),
+    (2, 512, 512),
+    (3, 0, 512),
+    (3, 512, 256),
+    (3, 768, 256),
 ]
 N_BLOCKS = len(BLOCKS)
 
@@ -89,7 +89,7 @@ def tile_offm_pa_t_kernel(tc, x, w1, b1, w2, b2, out):
         w2_scales = keep.tile([P, Z_GROUPS, C_OUT], U8, align_bytes=64)
 
         x_grouped, x_codes, x_scales = {}, {}, {}
-        z, z_codes, z_scales, planes, f_pairs = {}, {}, {}, {}, {}
+        z, z_codes, z_scales, planes = {}, {}, {}, {}
         y_bank, acc = {}, {}
         drained = set([])
 
@@ -105,7 +105,7 @@ def tile_offm_pa_t_kernel(tc, x, w1, b1, w2, b2, out):
             return BLOCKS[block][2]
 
         def load_x(block):
-            b, first, w = BLOCKS[block][:3]
+            b, first, w = BLOCKS[block]
             nc.sync.dma_start(out=x_raw[block][:], in_=x_rows[b][:, :, first : first + w])
 
         def load_w1(g):
@@ -176,52 +176,24 @@ def tile_offm_pa_t_kernel(tc, x, w1, b1, w2, b2, out):
                 z_scales[block] = zstage.tile([P, Z_GROUPS, w], U8, align_bytes=64, name="z_scales")
             return z[block]
 
-        def direct(block, h):
-            return h < BLOCKS[block][3]
-
         def hidden_f(block, h, j):
             if not live(block) or h * HALF >= width(block):
                 return
-            if direct(block, h):
-                y = y_psum.tile([P, PACK, QUAD], F32, name="y_quad", tag="y")
-                y_bank[(block, "f", h, j)] = y
-                first = h * HALF + j * QUAD
-                for a in range(PACK):
-                    hidden_pass(y[:, a, :], block, FMAP, a, slice(first, first + QUAD))
-                return
-            y = y_psum.tile([P, 2, HALF], F32, name="y_f", tag="y")
+            y = y_psum.tile([P, PACK, QUAD], F32, name="y_quad", tag="y")
             y_bank[(block, "f", h, j)] = y
-            for i in range(2):
-                hidden_pass(y[:, i, :], block, FMAP, 2 * j + i, slice(h * HALF, (h + 1) * HALF))
+            first = h * HALF + j * QUAD
+            for a in range(PACK):
+                hidden_pass(y[:, a, :], block, FMAP, a, slice(first, first + QUAD))
 
         def drain_f(block, h, j):
             if not live(block) or h * HALF >= width(block):
                 return
-            if direct(block, h):
-                first = h * HALF + j * QUAD
-                nc.vector.tensor_tensor(
-                    out=z_tiles(block)[:, FMAP, first : first + QUAD, :],
-                    in0=y_bank[(block, "f", h, j)][:].rearrange("p a n -> p n a"),
-                    in1=b1_f[:, FMAP, :].unsqueeze(1).to_broadcast([P, QUAD, PACK]),
-                    op=ADD,
-                )
-                return
-            if block not in f_pairs:
-                f_pairs[block] = zstage.tile([P, 2, width(block), 2], BF16, align_bytes=64, name="f_pairs")
+            first = h * HALF + j * QUAD
             nc.vector.tensor_tensor(
-                out=f_pairs[block][:, j, h * HALF : (h + 1) * HALF, :],
+                out=z_tiles(block)[:, FMAP, first : first + QUAD, :],
                 in0=y_bank[(block, "f", h, j)][:].rearrange("p a n -> p n a"),
-                in1=b1_f[:, FMAP, 2 * j : 2 * j + 2].unsqueeze(1).to_broadcast([P, HALF, 2]),
+                in1=b1_f[:, FMAP, :].unsqueeze(1).to_broadcast([P, QUAD, PACK]),
                 op=ADD,
-            )
-
-        def join_f(copy, block, h):
-            if not live(block) or h * HALF >= width(block) or direct(block, h):
-                return
-            cols = slice(h * HALF, (h + 1) * HALF)
-            copy(
-                out=z_tiles(block)[:, FMAP, cols, :].rearrange("p n (j i) -> p n j i", i=2),
-                in_=f_pairs[block][:, :, cols, :].rearrange("p j n i -> p n j i"),
             )
 
         def hidden_planes(block, g, a):
@@ -266,19 +238,11 @@ def tile_offm_pa_t_kernel(tc, x, w1, b1, w2, b2, out):
         def relu(block):
             if not live(block):
                 return
-            split = BLOCKS[block][3] * HALF
-            if split > 0:
-                nc.vector.tensor_scalar_max(
-                    out=z_tiles(block)[:, RELU, 0:split].rearrange("p n t -> p (n t)"),
-                    in0=z_tiles(block)[:, FMAP, 0:split].rearrange("p n t -> p (n t)"),
-                    scalar1=0.0,
-                )
-            if split < width(block):
-                nc.vector.tensor_scalar_max(
-                    out=z_tiles(block)[:, RELU, split:].rearrange("p n (j i) -> p n j i", i=2),
-                    in0=f_pairs[block][:, :, split:, :].rearrange("p j n i -> p n j i"),
-                    scalar1=0.0,
-                )
+            nc.vector.tensor_scalar_max(
+                out=z_tiles(block)[:, RELU].rearrange("p n t -> p (n t)"),
+                in0=z_tiles(block)[:, FMAP].rearrange("p n t -> p (n t)"),
+                scalar1=0.0,
+            )
 
         def quantise_z(block, g0, g1):
             if not live(block):
@@ -318,7 +282,7 @@ def tile_offm_pa_t_kernel(tc, x, w1, b1, w2, b2, out):
         def drain_output(block, m, engine):
             if not live(block):
                 return
-            b, first, w = BLOCKS[block][:3]
+            b, first, w = BLOCKS[block]
             result = ostage.tile([P, w], F32, name="result")
             if engine == "S":
                 nc.scalar.activation(
@@ -341,35 +305,36 @@ def tile_offm_pa_t_kernel(tc, x, w1, b1, w2, b2, out):
         for block in range(3, N_BLOCKS):
             load_x(block)
 
-        V_A = {WIDE: 192, HALF: 128}
-        X_S = {WIDE: 128, HALF: 64}
-        X_V = {WIDE: 128, HALF: 64}
+        def v_share(i):
+            return 224 if width(i) == WIDE else (HALF if i >= N_BLOCKS - 2 else 128)
+
+        def x_split(block):
+            w = width(block)
+            narrow = live(block - 2) and width(block - 2) < w
+            return (w // 4, w // 2 if narrow else w // 4)
+
 
         def gpsimd_x(block):
             if live(block):
                 w = width(block)
-                for first in range(X_V[w], w, 128):
-                    regroup_x(G, block, first, min(first + 128, w))
+                for first in range(x_split(block)[1], w, 192):
+                    regroup_x(G, block, first, min(first + 192, w))
 
         def scalar_x(block):
             if live(block):
-                regroup_x(S, block, 0, X_S[width(block)])
+                regroup_x(S, block, 0, x_split(block)[0])
 
         def vector_x(block):
             if live(block):
-                regroup_x(V, block, X_S[width(block)], X_V[width(block)])
+                regroup_x(V, block, x_split(block)[0], x_split(block)[1])
 
         def scalar_planes(i):
             if live(i):
-                regroup_planes(S, i, A, V_A[width(i)], width(i))
+                regroup_planes(S, i, A, v_share(i), width(i))
 
         def vector_planes(i):
             if live(i):
-                regroup_planes(V, i, A, 0, V_A[width(i)])
-
-        def join(i):
-            join_f(V, i, 0)
-            join_f(V, i, 1)
+                regroup_planes(V, i, A, 0, v_share(i))
 
         def round_(i):
             gpsimd_x(i + 2)
@@ -402,9 +367,8 @@ def tile_offm_pa_t_kernel(tc, x, w1, b1, w2, b2, out):
             hidden_f(i + 1, 1, 1)
             drain_output(i - 1, 3, "S")
             relu(i)
-            join(i)
-            quantise_z(i, RELU, RELU + 1)
             quantise_z(i, A, RELU)
+            quantise_z(i, RELU, RELU + 1)
             quantise_x(i + 2)
 
         with tc.manual_schedule():
@@ -435,7 +399,6 @@ def tile_offm_pa_t_kernel(tc, x, w1, b1, w2, b2, out):
             hidden_f(1, 0, 0)
             hidden_f(1, 0, 1)
             relu(0)
-            join_f(V, 0, 0)
             quantise_w2(A)
             regroup_x(S, 2, 256, WIDE)
             regroup_x(V, 2, 0, 256)
@@ -443,8 +406,8 @@ def tile_offm_pa_t_kernel(tc, x, w1, b1, w2, b2, out):
             regroup_w2(V, FMAP, 0, 2)
             regroup_w2(S, FMAP, 2, PACK)
             quantise_x(2)
-            quantise_z(0, RELU, RELU + 1)
             quantise_z(0, A, RELU)
+            quantise_z(0, RELU, RELU + 1)
             hidden_planes(2, A, 0)
             hidden_planes(2, A, 1)
             regroup_w2(V, RELU, 0, 2)
@@ -468,7 +431,6 @@ def tile_offm_pa_t_kernel(tc, x, w1, b1, w2, b2, out):
             drain_output(i - 1, 1, "S")
             output_bank(i - 1, 2)
             drain_output(i - 1, 2, "S")
-            join_f(V, i, 0)
             relu(i)
             output_bank(i - 1, 3)
             drain_output(i - 1, 3, "S")

@@ -78,7 +78,7 @@ def tile_offm_pa_t_kernel(tc, x, w1, b1, w2, b2, out):
         b2_bf = keep.tile([P, PACK], BF16)
         b1_f = keep.tile([P, Y_GROUPS, PACK], F32)
         b2_f = keep.tile([P, PACK], F32)
-        w1_raw = [keep.tile([P, PACK, K_PASS], BF16, name="w1_raw%d" % g) for g in range(Y_GROUPS)]
+        w1_raw = [[keep.tile([P, PACK, K_PASS // 2], BF16, name="w1_raw%d%d" % (g, h)) for h in range(2)] for g in range(Y_GROUPS)]
         w2_raw = [keep.tile([P, PACK, C_OUT], BF16, name="w2_raw%d" % g) for g in range(Z_GROUPS)]
         x_raw = [keep.tile([P, PACK, BLOCKS[i][2]], BF16, name="x_raw%d" % i) for i in range(N_BLOCKS)]
         w1_grouped = keep.tile([P, Y_GROUPS, PACK, P, PACK], BF16, align_bytes=64)
@@ -108,8 +108,9 @@ def tile_offm_pa_t_kernel(tc, x, w1, b1, w2, b2, out):
             b, first, w = BLOCKS[block]
             nc.sync.dma_start(out=x_raw[block][:], in_=x_rows[b][:, :, first : first + w])
 
-        def load_w1(g):
-            nc.sync.dma_start(out=w1_raw[g][:], in_=w1_rows[:, :, g * K_PASS : (g + 1) * K_PASS])
+        def load_w1(g, h):
+            first = g * K_PASS + h * K_PASS // 2
+            nc.sync.dma_start(out=w1_raw[g][h][:], in_=w1_rows[:, :, first : first + K_PASS // 2])
 
         def load_w2(g):
             nc.sync.dma_start(out=w2_raw[g][:], in_=w2_rows[g])
@@ -136,8 +137,9 @@ def tile_offm_pa_t_kernel(tc, x, w1, b1, w2, b2, out):
                 in_=x_grouped[block][:].rearrange("p n t -> p (n t)"),
             )
 
-        def regroup_w1(copy, g, first, last):
-            regroup_weight(copy, w1_grouped[:, g], w1_raw[g][:], first, last)
+        def regroup_w1(copy, g, h, first, last):
+            half = slice(h * P // 2, (h + 1) * P // 2)
+            regroup_weight(copy, w1_grouped[:, g, :, half, :], w1_raw[g][h][:], first, last)
 
         def regroup_w2(copy, g, first, last):
             if first < last:
@@ -292,9 +294,11 @@ def tile_offm_pa_t_kernel(tc, x, w1, b1, w2, b2, out):
                 nc.vector.tensor_scalar_add(out=result[:], in0=acc[(block, m)][:], scalar1=b2_f[:, m : m + 1])
             nc.sync.dma_start(out=out_rows[b][:, m, first : first + w], in_=result[:])
 
-        load_w1(A)
+        load_w1(A, 0)
+        load_w1(A, 1)
         load_x(0)
-        load_w1(FMAP)
+        load_w1(FMAP, 0)
+        load_w1(FMAP, 1)
         nc.sync.dma_start(out=b1_bf[:], in_=b1.rearrange("(g p a) -> p g a", g=Y_GROUPS, a=PACK))
         load_x(1)
         load_w2(A)
@@ -305,20 +309,22 @@ def tile_offm_pa_t_kernel(tc, x, w1, b1, w2, b2, out):
         for block in range(3, N_BLOCKS):
             load_x(block)
 
+        G_PIXELS = {WIDE: 320, HALF: 160}
+
         def v_share(i):
-            return 224 if width(i) == WIDE else (HALF if i >= N_BLOCKS - 2 else 128)
+            return 256 if width(i) == WIDE else (HALF if i >= N_BLOCKS - 2 else 128)
 
         def x_split(block):
             w = width(block)
-            narrow = live(block - 2) and width(block - 2) < w
-            return (w // 4, w // 2 if narrow else w // 4)
+            gpsimd = min(w - w // 4, G_PIXELS[width(block - 2)])
+            return w // 4, w - gpsimd
 
 
         def gpsimd_x(block):
             if live(block):
                 w = width(block)
-                for first in range(x_split(block)[1], w, 192):
-                    regroup_x(G, block, first, min(first + 192, w))
+                for first in range(x_split(block)[1], w, 160):
+                    regroup_x(G, block, first, min(first + 160, w))
 
         def scalar_x(block):
             if live(block):
@@ -372,15 +378,17 @@ def tile_offm_pa_t_kernel(tc, x, w1, b1, w2, b2, out):
             quantise_x(i + 2)
 
         with tc.manual_schedule():
-            regroup_w1(V, A, 0, 2)
-            regroup_w1(S, A, 2, PACK)
+            for h in range(2):
+                regroup_w1(V, A, h, 0, 2)
+                regroup_w1(S, A, h, 2, PACK)
             regroup_x(V, 0, 0, HALF)
             quantise_w1(A)
             quantise_x(0)
             hidden_planes(0, A, 0)
             hidden_planes(0, A, 2)
-            regroup_w1(V, FMAP, 0, 2)
-            regroup_w1(S, FMAP, 2, PACK)
+            for h in range(2):
+                regroup_w1(V, FMAP, h, 0, 2)
+                regroup_w1(S, FMAP, h, 2, PACK)
             nc.vector.tensor_copy(out=b1_f[:], in_=b1_bf[:])
             regroup_x(V, 1, 0, HALF)
             quantise_w1(FMAP)
@@ -391,6 +399,7 @@ def tile_offm_pa_t_kernel(tc, x, w1, b1, w2, b2, out):
             drain_planes(0, A, 2)
             regroup_w2(V, A, 0, 1)
             regroup_w2(S, A, 1, PACK)
+            regroup_x(G, 2, 0, 128)
             drain_f(0, 0, 0)
             hidden_planes(1, A, 0)
             hidden_planes(1, A, 2)
@@ -401,7 +410,7 @@ def tile_offm_pa_t_kernel(tc, x, w1, b1, w2, b2, out):
             relu(0)
             quantise_w2(A)
             regroup_x(S, 2, 256, WIDE)
-            regroup_x(V, 2, 0, 256)
+            regroup_x(V, 2, 128, 256)
             drain_planes(1, A, 0)
             regroup_w2(V, FMAP, 0, 2)
             regroup_w2(S, FMAP, 2, PACK)

from contextlib import ExitStack

import concourse.mybir as mybir

BF16 = mybir.dt.bfloat16
F32 = mybir.dt.float32
U32 = mybir.dt.uint32
U8 = mybir.dt.uint8
FP8X4 = mybir.dt.float8_e4m3fn_x4
ADD = mybir.AluOpType.add
MULT = mybir.AluOpType.mult
IDENTITY = mybir.ActivationFunctionType.Identity

P = 128
PACK = 4
K_PASS = P * PACK

C_IN = 512
HIDDEN = 1024
PIXELS = 1024
IMAGES = 4
C_OUT = 512
Y_GROUPS = HIDDEN // K_PASS
Z_GROUPS = Y_GROUPS + 1
A, FMAP, RELU = 0, 1, 2
WIDE = 512
HALF = WIDE // 2
QUAD = WIDE // PACK

BLOCKS = [
    (0, 0, 256),
    (0, 256, 256),
    (0, 512, 512),
    (1, 0, 512),
    (1, 512, 512),
    (2, 0, 512),
    (2, 512, 512),
    (3, 0, 512),
    (3, 512, 256),
    (3, 768, 256),
]
N_BLOCKS = len(BLOCKS)

FLOPS = 2 * IMAGES * PIXELS * (C_IN * HIDDEN + Z_GROUPS * K_PASS * C_OUT)


def regroup_pixels(copy, grouped, rows):
    copy(
        out=grouped.rearrange("p (c i) t -> p c t i", i=PACK),
        in_=rows.rearrange("p t (c i) -> p c t i", i=PACK),
    )


def regroup_weight(copy, grouped, rows, first, last):
    copy(
        out=grouped[:, first:last].rearrange("p a q t -> p q t a"),
        in_=rows.rearrange("p t (q a) -> p q t a", a=PACK)[:, :, :, first:last],
    )


def tile_offm_pa_t_kernel(tc, x, w1, b1, w2, b2, out):
    nc = tc.nc
    with ExitStack() as ctx:
        keep = ctx.enter_context(tc.tile_pool(name="keep", bufs=1))
        xg = ctx.enter_context(tc.tile_pool(name="xg", bufs=1))
        xstage = ctx.enter_context(tc.tile_pool(name="xstage", bufs=2))
        zstage = ctx.enter_context(tc.tile_pool(name="zstage", bufs=3))
        ostage = ctx.enter_context(tc.tile_pool(name="ostage", bufs=8))
        y_psum = ctx.enter_context(tc.psum_pool(name="y_psum", bufs=5))
        o_psum = ctx.enter_context(tc.psum_pool(name="o_psum", bufs=3))

        x_rows = x.rearrange("b (p t) h w -> b p t (h w)", t=PACK)
        w1_rows = w1.rearrange("(p t) d -> p t d", t=PACK)
        w2_rows = w2.rearrange("(g p t) e -> g p t e", g=Z_GROUPS, t=PACK)
        out_rows = out.rearrange("b (p m) h w -> b p m (h w)", m=PACK)

        b1_bf = keep.tile([P, Y_GROUPS, PACK], BF16)
        b2_bf = keep.tile([P, PACK], BF16)
        b1_f = keep.tile([P, Y_GROUPS, PACK], F32)
        b2_f = keep.tile([P, PACK], F32)
        w1_raw = [[keep.tile([P, PACK, K_PASS // 2], BF16, name="w1_raw%d%d" % (g, h)) for h in range(2)] for g in range(Y_GROUPS)]
        w2_raw = [keep.tile([P, PACK, C_OUT], BF16, name="w2_raw%d" % g) for g in range(Z_GROUPS)]
        x_raw = [keep.tile([P, PACK, BLOCKS[i][2]], BF16, name="x_raw%d" % i) for i in range(N_BLOCKS)]
        w1_grouped = keep.tile([P, Y_GROUPS, PACK, P, PACK], BF16, align_bytes=64)
        w2_grouped = keep.tile([P, Z_GROUPS, PACK, P, PACK], BF16, align_bytes=64)
        w1_codes = keep.tile([P, Y_GROUPS, K_PASS], U32, align_bytes=64)
        w1_scales = keep.tile([P, Y_GROUPS, K_PASS], U8, align_bytes=64)
        w2_codes = keep.tile([P, Z_GROUPS, C_OUT], U32, align_bytes=64)
        w2_scales = keep.tile([P, Z_GROUPS, C_OUT], U8, align_bytes=64)

        x_grouped, x_codes, x_scales = {}, {}, {}
        z, z_codes, z_scales, planes = {}, {}, {}, {}
        y_bank, acc = {}, {}
        drained = set([])

        V, S = nc.vector.tensor_copy, nc.scalar.copy

        def G(out, in_):
            nc.gpsimd.tensor_scalar(out=out, in0=in_, scalar1=1.0, scalar2=0.0, op0=MULT, op1=ADD)

        def live(block):
            return 0 <= block < N_BLOCKS

        def width(block):
            return BLOCKS[block][2]

        def load_x(block):
            b, first, w = BLOCKS[block]
            nc.sync.dma_start(out=x_raw[block][:], in_=x_rows[b][:, :, first : first + w])

        def load_w1(g, h):
            first = g * K_PASS + h * K_PASS // 2
            nc.sync.dma_start(out=w1_raw[g][h][:], in_=w1_rows[:, :, first : first + K_PASS // 2])

        def load_w2(g):
            nc.sync.dma_start(out=w2_raw[g][:], in_=w2_rows[g])

        def regroup_x(copy, block, first, last):
            if not live(block) or first >= last:
                return
            if block not in x_grouped:
                x_grouped[block] = xg.tile([P, width(block), PACK], BF16, align_bytes=64, name="x_grouped")
            cols = slice(first, last)
            if copy is G:
                G(out=x_grouped[block][:, cols, :], in_=x_raw[block][:, :, cols].rearrange("p t n -> p n t"))
            else:
                regroup_pixels(copy, x_grouped[block][:, cols, :], x_raw[block][:, :, cols])

        def quantise_x(block):
            if not live(block):
                return
            x_codes[block] = xstage.tile([P, width(block)], U32, align_bytes=64, name="x_codes")
            x_scales[block] = xstage.tile([P, width(block)], U8, align_bytes=64, name="x_scales")
            nc.vector.quantize_mx(
                out=x_codes[block][:].bitcast(FP8X4),
                scales=x_scales[block][:],
                in_=x_grouped[block][:].rearrange("p n t -> p (n t)"),
            )

        def regroup_w1(copy, g, h, first, last):
            half = slice(h * P // 2, (h + 1) * P // 2)
            regroup_weight(copy, w1_grouped[:, g, :, half, :], w1_raw[g][h][:], first, last)

        def regroup_w2(copy, g, first, last):
            if first < last:
                regroup_weight(copy, w2_grouped[:, g], w2_raw[g][:], first, last)

        def quantise_weight(grouped, codes, scales, g):
            nc.vector.quantize_mx(
                out=codes[:, g, :].bitcast(FP8X4),
                scales=scales[:, g, :],
                in_=grouped[:, g].rearrange("p a q t -> p (a q t)"),
            )

        def quantise_w1(g):
            quantise_weight(w1_grouped, w1_codes, w1_scales, g)

        def quantise_w2(g):
            quantise_weight(w2_grouped, w2_codes, w2_scales, g)

        def hidden_pass(y_part, block, g, a, cols):
            w_cols = slice(a * P, (a + 1) * P)
            nc.tensor.matmul_mx(
                out=y_part,
                lhsT=w1_codes[:, g, w_cols].bitcast(FP8X4),
                lhsT_scale=w1_scales[:, g, w_cols],
                rhs=x_codes[block][:, cols].bitcast(FP8X4),
                rhs_scale=x_scales[block][:, cols],
                start=True,
                stop=True,
            )

        def z_tiles(block):
            if block not in z:
                w = width(block)
                z[block] = zstage.tile([P, Z_GROUPS, w, PACK], BF16, align_bytes=64, name="z")
                z_codes[block] = zstage.tile([P, Z_GROUPS, w], U32, align_bytes=64, name="z_codes")
                z_scales[block] = zstage.tile([P, Z_GROUPS, w], U8, align_bytes=64, name="z_scales")
            return z[block]

        def hidden_f(block, h, j):
            if not live(block) or h * HALF >= width(block):
                return
            y = y_psum.tile([P, PACK, QUAD], F32, name="y_quad", tag="y")
            y_bank[(block, "f", h, j)] = y
            first = h * HALF + j * QUAD
            for a in range(PACK):
                hidden_pass(y[:, a, :], block, FMAP, a, slice(first, first + QUAD))

        def drain_f(block, h, j):
            if not live(block) or h * HALF >= width(block):
                return
            first = h * HALF + j * QUAD
            nc.vector.tensor_tensor(
                out=z_tiles(block)[:, FMAP, first : first + QUAD, :],
                in0=y_bank[(block, "f", h, j)][:].rearrange("p a n -> p n a"),
                in1=b1_f[:, FMAP, :].unsqueeze(1).to_broadcast([P, QUAD, PACK]),
                op=ADD,
            )

        def hidden_planes(block, g, a):
            if not live(block) or (block, g, a) in y_bank:
                return
            w = width(block)
            per_bank = WIDE // w
            if a % per_bank:
                return
            y = y_psum.tile([P, per_bank, w], F32, name="y_planes", tag="y")
            for i in range(per_bank):
                y_bank[(block, g, a + i)] = y[:, i, :]
                hidden_pass(y[:, i, :], block, g, a + i, slice(0, w))

        def drain_planes(block, g, a, engine="S"):
            if not live(block) or (block, g, a) in drained:
                return
            drained.add((block, g, a))
            store = planes
            w = width(block)
            if block not in store:
                store[block] = zstage.tile([P, PACK, w], BF16, name="planes")
            per_bank = WIDE // w
            if a % per_bank:
                return
            for i in range(a, a + per_bank):
                if engine == "S":
                    nc.scalar.activation(
                        out=store[block][:, i, :], in_=y_bank[(block, g, i)], func=IDENTITY,
                        bias=b1_f[:, g, i : i + 1], scale=1.0,
                    )
                else:
                    nc.vector.tensor_scalar_add(
                        out=store[block][:, i, :], in0=y_bank[(block, g, i)], scalar1=b1_f[:, g, i : i + 1]
                    )

        def regroup_planes(copy, block, g, first, last):
            if not live(block) or first >= last:
                return
            regroup_pixels(copy, z_tiles(block)[:, g, first:last, :], planes[block][:, :, first:last])

        def relu(block):
            if not live(block):
                return
            nc.vector.tensor_scalar_max(
                out=z_tiles(block)[:, RELU].rearrange("p n t -> p (n t)"),
                in0=z_tiles(block)[:, FMAP].rearrange("p n t -> p (n t)"),
                scalar1=0.0,
            )

        def quantise_z(block, g0, g1):
            if not live(block):
                return
            nc.vector.quantize_mx(
                out=z_codes[block][:, g0:g1, :].rearrange("p g n -> p (g n)").bitcast(FP8X4),
                scales=z_scales[block][:, g0:g1, :].rearrange("p g n -> p (g n)"),
                in_=z[block][:, g0:g1].rearrange("p g n t -> p (g n t)"),
            )

        def output_pass(block, g, m):
            w_cols = slice(m * P, (m + 1) * P)
            nc.tensor.matmul_mx(
                out=acc[(block, m)][:],
                lhsT=w2_codes[:, g, w_cols].bitcast(FP8X4),
                lhsT_scale=w2_scales[:, g, w_cols],
                rhs=z_codes[block][:, g, :].bitcast(FP8X4),
                rhs_scale=z_scales[block][:, g, :],
                start=(g == 0),
                stop=(g == Z_GROUPS - 1),
            )

        def output_bank(block, m):
            if not live(block):
                return
            acc[(block, m)] = o_psum.tile([P, width(block)], F32, name="acc")
            for g in range(Z_GROUPS):
                output_pass(block, g, m)

        def output_group_last(g):
            block = N_BLOCKS - 1
            for m in range(PACK):
                if g == 0:
                    acc[(block, m)] = y_psum.tile([P, width(block)], F32, name="acc_last", tag="y")
                output_pass(block, g, m)

        def drain_output(block, m, engine):
            if not live(block):
                return
            b, first, w = BLOCKS[block]
            result = ostage.tile([P, w], F32, name="result")
            if engine == "S":
                nc.scalar.activation(
                    out=result[:], in_=acc[(block, m)][:], func=IDENTITY, bias=b2_f[:, m : m + 1], scale=1.0
                )
            else:
                nc.vector.tensor_scalar_add(out=result[:], in0=acc[(block, m)][:], scalar1=b2_f[:, m : m + 1])
            nc.sync.dma_start(out=out_rows[b][:, m, first : first + w], in_=result[:])

        load_w1(A, 0)
        load_w1(A, 1)
        load_x(0)
        load_w1(FMAP, 0)
        load_w1(FMAP, 1)
        nc.sync.dma_start(out=b1_bf[:], in_=b1.rearrange("(g p a) -> p g a", g=Y_GROUPS, a=PACK))
        load_x(1)
        load_w2(A)
        load_x(2)
        load_w2(FMAP)
        load_w2(RELU)
        nc.sync.dma_start(out=b2_bf[:], in_=b2.rearrange("(p m) -> p m", m=PACK))
        for block in range(3, N_BLOCKS):
            load_x(block)

        G_PIXELS = {WIDE: 320, HALF: 160}

        def v_share(i):
            return 256 if width(i) == WIDE else (HALF if i >= N_BLOCKS - 2 else 128)

        def x_split(block):
            w = width(block)
            gpsimd = min(w - w // 4, G_PIXELS[width(block - 2)])
            return w // 4, w - gpsimd


        def gpsimd_x(block):
            if live(block):
                w = width(block)
                for first in range(x_split(block)[1], w, 160):
                    regroup_x(G, block, first, min(first + 160, w))

        def scalar_x(block):
            if live(block):
                regroup_x(S, block, 0, x_split(block)[0])

        def vector_x(block):
            if live(block):
                regroup_x(V, block, x_split(block)[0], x_split(block)[1])

        def scalar_planes(i):
            if live(i):
                regroup_planes(S, i, A, v_share(i), width(i))

        def vector_planes(i):
            if live(i):
                regroup_planes(V, i, A, 0, v_share(i))

        def round_(i):
            gpsimd_x(i + 2)
            scalar_planes(i)
            drain_f(i, 0, 0)
            output_bank(i - 1, 0)
            hidden_planes(i + 1, A, 0)
            drain_f(i, 0, 1)
            hidden_planes(i + 1, A, 1)
            drain_output(i - 1, 0, "S")
            drain_planes(i + 1, A, 0)
            drain_f(i, 1, 0)
            output_bank(i - 1, 1)
            hidden_planes(i + 1, A, 2)
            drain_planes(i + 1, A, 1)
            drain_output(i - 1, 1, "S")
            drain_f(i, 1, 1)
            hidden_planes(i + 1, A, 3)
            drain_planes(i + 1, A, 2)
            vector_planes(i)
            vector_x(i + 2)
            output_bank(i - 1, 2)
            scalar_x(i + 2)
            hidden_f(i + 1, 0, 0)
            drain_planes(i + 1, A, 3)
            hidden_f(i + 1, 0, 1)
            drain_output(i - 1, 2, "S")
            output_bank(i - 1, 3)
            hidden_f(i + 1, 1, 0)
            hidden_f(i + 1, 1, 1)
            drain_output(i - 1, 3, "S")
            relu(i)
            quantise_z(i, A, RELU)
            quantise_z(i, RELU, RELU + 1)
            quantise_x(i + 2)

        with tc.manual_schedule():
            for h in range(2):
                regroup_w1(V, A, h, 0, 2)
                regroup_w1(S, A, h, 2, PACK)
            regroup_x(V, 0, 0, HALF)
            quantise_w1(A)
            quantise_x(0)
            hidden_planes(0, A, 0)
            hidden_planes(0, A, 2)
            for h in range(2):
                regroup_w1(V, FMAP, h, 0, 2)
                regroup_w1(S, FMAP, h, 2, PACK)
            nc.vector.tensor_copy(out=b1_f[:], in_=b1_bf[:])
            regroup_x(V, 1, 0, HALF)
            quantise_w1(FMAP)
            quantise_x(1)
            hidden_f(0, 0, 0)
            hidden_f(0, 0, 1)
            drain_planes(0, A, 0)
            drain_planes(0, A, 2)
            regroup_w2(V, A, 0, 1)
            regroup_w2(S, A, 1, PACK)
            regroup_x(G, 2, 0, 128)
            drain_f(0, 0, 0)
            hidden_planes(1, A, 0)
            hidden_planes(1, A, 2)
            drain_f(0, 0, 1)
            regroup_planes(V, 0, A, 0, HALF)
            hidden_f(1, 0, 0)
            hidden_f(1, 0, 1)
            relu(0)
            quantise_w2(A)
            regroup_x(S, 2, 256, WIDE)
            regroup_x(V, 2, 128, 256)
            drain_planes(1, A, 0)
            regroup_w2(V, FMAP, 0, 2)
            regroup_w2(S, FMAP, 2, PACK)
            quantise_x(2)
            quantise_z(0, A, RELU)
            quantise_z(0, RELU, RELU + 1)
            hidden_planes(2, A, 0)
            hidden_planes(2, A, 1)
            regroup_w2(V, RELU, 0, 2)
            regroup_w2(S, RELU, 2, PACK)
            drain_planes(1, A, 2)
            quantise_w2(FMAP)
            nc.vector.tensor_copy(out=b2_f[:], in_=b2_bf[:])
            drain_planes(2, A, 0)
            quantise_w2(RELU)
            for i in range(1, N_BLOCKS - 1):
                round_(i)
            i = N_BLOCKS - 1
            scalar_planes(i)
            vector_planes(i)
            output_bank(i - 1, 0)
            drain_f(i, 0, 0)
            drain_output(i - 1, 0, "S")
            drain_f(i, 0, 1)
            output_bank(i - 1, 1)
            quantise_z(i, A, FMAP)
            drain_output(i - 1, 1, "S")
            output_bank(i - 1, 2)
            drain_output(i - 1, 2, "S")
            relu(i)
            output_bank(i - 1, 3)
            drain_output(i - 1, 3, "S")
            output_group_last(A)
            quantise_z(i, FMAP, RELU)
            output_group_last(FMAP)
            quantise_z(i, RELU, RELU + 1)
            output_group_last(RELU)
            for m in range(PACK):
                drain_output(i, m, "VS"[m % 2])
